import numpy as np
import ml_dtypes


def mxq(x, axis, fmt="e4m3"):
    dtype, down = {"e4m3": (ml_dtypes.float8_e4m3fn, 7), "e5m2": (ml_dtypes.float8_e5m2, 14)}[fmt]
    v = np.moveaxis(np.asarray(x, np.float32).astype(ml_dtypes.bfloat16).astype(np.float64), axis, -1)
    blocks = v.reshape(v.shape[:-1] + (-1, 32))
    amax = np.abs(blocks).max(-1, keepdims=True)
    byte = np.maximum(np.where(amax > 0, np.frexp(amax)[1] - 1 + 127, 0) - down, 1)
    scale = np.exp2(byte - 127.0)
    codes = (blocks / scale).astype(np.float32).astype(dtype).astype(np.float64)
    return np.moveaxis((codes * scale).reshape(v.shape), -1, axis)


WIDE = False


def mx_kscale(k):
    if not WIDE:
        return np.ones(k)
    levels = np.array([10, -10, 5, -5, 0])
    a = np.random.permutation(np.resize(levels, k // 512 * 4)).reshape(k // 512, 4)
    idx = np.arange(k)
    return np.exp2(a[idx // 512, idx % 128 // 32])


BF16 = ml_dtypes.bfloat16


def bf(x):
    return np.asarray(x, np.float32).astype(BF16)


def f64(x):
    return np.asarray(x).astype(np.float64)


E2M1 = np.array([0.0, 0.5, 1.0, 1.5, 2.0, 3.0, 4.0, 6.0, -0.0, -0.5, -1.0, -1.5, -2.0, -3.0, -4.0, -6.0])


def pack_weight(w, fmt):
    k, n = w.shape
    w = f64(bf(w)).reshape(k // 32, 32, n)
    amax = np.abs(w).max(1)
    if fmt == "e4m3":
        byte = np.frexp(amax)[1] - 1 + 127 - 7
    else:
        mant, ex = np.frexp(amax / 6.0)
        byte = np.where(mant > 0.5, ex, ex - 1) + 127
    byte = np.clip(np.where(amax > 0, byte, 1), 1, 254)
    scaled = (w * np.exp2(127.0 - byte)[:, None, :]).reshape(k, n).astype(np.float32)
    by_word = np.ascontiguousarray(scaled.reshape(k // 512, 128, 4, n).transpose(0, 1, 3, 2))
    if fmt == "e4m3":
        words = by_word.astype(ml_dtypes.float8_e4m3fn).view(np.uint8)
    else:
        c = by_word.astype(ml_dtypes.float4_e2m1fn).view(np.uint8) & 0xF
        words = c[..., 0::2] | (c[..., 1::2] << 4)
    return np.ascontiguousarray(words), np.ascontiguousarray(byte.astype(np.uint8).reshape(k // 512, 16, n))


def unpack_weight(words, scales, fmt):
    g, p, n, _ = words.shape
    if fmt == "e4m3":
        vals = np.ascontiguousarray(words).view(ml_dtypes.float8_e4m3fn).astype(np.float64)
    else:
        nib = np.empty((g, p, n, 4), np.uint8)
        nib[..., 0::2] = words & 0xF
        nib[..., 1::2] = words >> 4
        vals = E2M1[nib]
    vals = vals * np.repeat(np.exp2(scales.astype(np.float64) - 127.0), 8, axis=1)[..., None]
    return vals.transpose(0, 1, 3, 2).reshape(g * 512, n)


B, C, D, H, W, W0, W1 = 16, 512, 128, 16, 32, 64, 256
N = H * W
FMT = "e4m3"


def setup_inputs():
    s = mx_kscale(C)
    x = bf(np.random.standard_normal((B, C, N)))
    out1 = bf(np.random.standard_normal((B, C, N)) * 0.6 * s[None, :, None])
    q = bf(np.random.standard_normal((B, N, D)) * 0.42)
    k = bf(np.random.standard_normal((B, D, N)) * 0.42)
    wv2 = np.random.standard_normal((C, C)) * 4.0 / np.sqrt(C) / s[None, :]
    wv2_words, wv2_scales = pack_weight(np.ascontiguousarray(wv2.T), FMT)
    bv2 = bf(np.random.standard_normal(C) * 0.3)
    gamma = bf(1.0 + 0.1 * np.random.standard_normal(1))
    return {
        "x": x,
        "out1": out1,
        "q": q,
        "k": k,
        "wv2_words": wv2_words,
        "wv2_scales": wv2_scales,
        "bv2": bv2,
        "gamma": gamma,
    }


def reference(x, out1, q, k, wv2_words, wv2_scales, bv2, gamma):
    val = (unpack_weight(wv2_words, wv2_scales, FMT).T @ mxq(f64(out1), 1, "e4m3")) + f64(bv2)[None, :, None]
    s = f64(q) @ f64(k)
    e = np.exp(s - s.max(-1, keepdims=True))
    out = (mxq(val, 2, "e4m3") @ mxq(e, 2, "e4m3").transpose(0, 2, 1)) / e.sum(-1)[:, None, :]
    return f64(gamma)[0] * out + f64(x)

@@ -1,0 +1,253 @@
+from contextlib import ExitStack
+
+import concourse.mybir as mybir
+from concourse.masks import make_identity
+
+BF16 = mybir.dt.bfloat16
+F32 = mybir.dt.float32
+I32 = mybir.dt.int32
+U32 = mybir.dt.uint32
+U8 = mybir.dt.uint8
+FP8X4 = mybir.dt.float8_e4m3fn_x4
+ACT = mybir.ActivationFunctionType
+ALU = mybir.AluOpType
+AXIS = mybir.AxisListType
+
+B = 16
+C = 512
+N = 512
+D = 128
+P = 128
+PACK = 4
+BLOCKS = C // P
+PAIR = 2
+PREFETCH = 2
+
+FLOPS = 2 * B * (C * C * N + N * D * N + C * N * N)
+
+
+def block(i):
+    return slice(i * P, (i + 1) * P)
+
+
+def tile_mvpam_module_mask_cascade_pb_t_kernel(
+    tc, x, out1, q, k, wv2_words, wv2_scales, bv2, gamma, out
+):
+    nc = tc.nc
+    with ExitStack() as ctx:
+        const = ctx.enter_context(tc.tile_pool(name="const", bufs=1))
+        loads = ctx.enter_context(tc.tile_pool(name="loads", bufs=PREFETCH + 1))
+        residual = ctx.enter_context(tc.tile_pool(name="residual", bufs=PREFETCH + 3))
+        work = ctx.enter_context(tc.tile_pool(name="work", bufs=2))
+        results = ctx.enter_context(tc.tile_pool(name="results", bufs=4))
+        psum_mm = ctx.enter_context(tc.psum_pool(name="psum_mm", bufs=5))
+        psum_tr = ctx.enter_context(tc.psum_pool(name="psum_tr", bufs=3))
+
+        w_codes = const.tile([P, C], U32, align_bytes=64)
+        nc.sync.dma_start(
+            out=w_codes[:].bitcast(I32),
+            in_=wv2_words[0].rearrange("p c t -> p (c t)").bitcast(I32),
+        )
+        w_scales = const.tile([P, C], U8, align_bytes=64)
+        nc.vector.memset(w_scales[:].bitcast(I32), 0)
+        for quadrant in range(4):
+            nc.sync.dma_start(
+                out=w_scales[32 * quadrant : 32 * quadrant + 4, :].bitcast(I32),
+                in_=wv2_scales[0, 4 * quadrant : 4 * quadrant + 4, :].bitcast(I32),
+            )
+
+        ident_bf16 = const.tile([P, P], BF16)
+        make_identity(nc, ident_bf16[:])
+        ident_f32 = const.tile([P, P], F32)
+        make_identity(nc, ident_f32[:])
+
+        bias_rows = const.tile([P, P], BF16)
+        nc.vector.memset(bias_rows[:], 0.0)
+        nc.sync.dma_start(out=bias_rows[0:BLOCKS, :], in_=bv2.rearrange("(cb p) -> cb p", p=P))
+        bias_ps = psum_tr.tile([P, P], BF16, tag="tr")
+        nc.tensor.transpose(out=bias_ps[:], in_=bias_rows[:], identity=ident_bf16[:])
+        bias_col = const.tile([P, BLOCKS], F32)
+        nc.vector.tensor_copy(out=bias_col[:], in_=bias_ps[:, 0:BLOCKS])
+
+        gamma_bf16 = const.tile([P, 1], BF16)
+        nc.sync.dma_start(out=gamma_bf16[:], in_=gamma.partition_broadcast(P))
+        gamma_col = const.tile([P, 1], F32)
+        nc.vector.tensor_copy(out=gamma_col[:], in_=gamma_bf16[:])
+
+        live = {}
+
+        def load(b):
+            q_sb = loads.tile([P, BLOCKS, D], BF16)
+            nc.sync.dma_start(out=q_sb[:], in_=q[b].rearrange("(mb p) d -> p mb d", p=P))
+            k_sb = loads.tile([D, N], BF16)
+            nc.sync.dma_start(out=k_sb[:], in_=k[b])
+            o1_raw = loads.tile([P, PACK, N], BF16)
+            nc.sync.dma_start(out=o1_raw[:], in_=out1[b].rearrange("(p j) n -> p j n", j=PACK))
+            x_sb = residual.tile([P, BLOCKS, N], BF16)
+            nc.sync.dma_start(out=x_sb[:], in_=x[b].rearrange("(cb p) m -> p cb m", p=P))
+            live[b] = {"q": q_sb, "k": k_sb, "o1": o1_raw, "x": x_sb}
+
+        def transpose_queries(b):
+            qT_ps = psum_tr.tile([D, N], BF16, tag="tr")
+            for mb in range(BLOCKS):
+                nc.tensor.transpose(
+                    out=qT_ps[:, block(mb)], in_=live[b]["q"][:, mb, :], identity=ident_bf16[:]
+                )
+            qT_sb = work.tile([D, N], BF16)
+            nc.scalar.copy(out=qT_sb[:], in_=qT_ps[:])
+            live[b]["qT"] = qT_sb
+
+        def quantise_out1(b):
+            o1_grouped = work.tile([P, N, PACK], BF16, align_bytes=64)
+            nc.vector.tensor_copy(
+                out=o1_grouped[:].rearrange("p (c i) j -> p c j i", i=4),
+                in_=live[b]["o1"][:].rearrange("p j (c i) -> p c j i", i=4),
+            )
+            o1_codes = work.tile([P, N], U32, align_bytes=64)
+            o1_scales = work.tile([P, N], U8, align_bytes=64)
+            nc.vector.quantize_mx(
+                out=o1_codes[:].bitcast(FP8X4),
+                scales=o1_scales[:],
+                in_=o1_grouped[:].rearrange("p n j -> p (n j)"),
+            )
+            live[b]["o1_codes"] = o1_codes
+            live[b]["o1_scales"] = o1_scales
+
+        def begin_scores_and_values(b):
+            live[b]["neg_max"] = work.tile([P, BLOCKS], F32, name="neg_max")
+            live[b]["row_sum"] = work.tile([P, BLOCKS], F32, name="row_sum")
+            live[b]["e"] = work.tile([P, BLOCKS, N], BF16, name="e_sb")
+            live[b]["val"] = work.tile([P, BLOCKS, N], BF16, name="val_sb")
+
+        def scores(b, mb):
+            neg_max = live[b]["neg_max"][:, mb : mb + 1]
+            s_ps = psum_mm.tile([P, N], F32, tag="mm")
+            nc.tensor.matmul(
+                out=s_ps[:],
+                lhsT=live[b]["qT"][:, block(mb)],
+                rhs=live[b]["k"][:],
+                start=True,
+                stop=True,
+            )
+            nc.vector.tensor_reduce(out=neg_max, in_=s_ps[:], axis=AXIS.X, op=ALU.max, negate=True)
+            nc.scalar.activation(
+                out=live[b]["e"][:, mb, :],
+                in_=s_ps[:],
+                func=ACT.Exp,
+                bias=neg_max,
+                scale=1.0,
+                accum_out=live[b]["row_sum"][:, mb : mb + 1],
+            )
+
+        def values(b, cb):
+            val_ps = psum_mm.tile([P, N], F32, tag="mm")
+            nc.tensor.matmul_mx(
+                out=val_ps[:],
+                lhsT=w_codes[:, block(cb)].bitcast(FP8X4),
+                lhsT_scale=w_scales[:, block(cb)],
+                rhs=live[b]["o1_codes"][:].bitcast(FP8X4),
+                rhs_scale=live[b]["o1_scales"][:],
+                start=True,
+                stop=True,
+            )
+            nc.scalar.activation(
+                out=live[b]["val"][:, cb, :],
+                in_=val_ps[:],
+                func=ACT.Identity,
+                bias=bias_col[:, cb : cb + 1],
+                scale=1.0,
+            )
+
+        def keys_to_partitions(rows_sb, label):
+            grouped = work.tile([P, C, PACK], BF16, align_bytes=64, name=label + "_grouped")
+            grouped_words = (
+                grouped[:]
+                .rearrange("p r t -> p (r t)")
+                .bitcast(F32)
+                .rearrange("p (r u) -> p r u", u=PAIR)
+            )
+            for half in range(BLOCKS // 2):
+                words_ps = psum_tr.tile([P, 2, PAIR, P], F32, tag="tr")
+                for i in range(2):
+                    row_words = rows_sb[:, 2 * half + i, :].bitcast(F32)
+                    for u in range(PAIR):
+                        nc.tensor.transpose(
+                            out=words_ps[:, i, u, :], in_=row_words[:, block(u)], identity=ident_f32[:]
+                        )
+                nc.scalar.copy(
+                    out=grouped_words[:, 2 * half * P : (2 * half + 2) * P, :].rearrange(
+                        "p (i r) u -> p i r u", i=2
+                    ),
+                    in_=words_ps[:].rearrange("p i u r -> p i r u"),
+                )
+            return grouped
+
+        def quantise_along_keys(grouped, label):
+            codes = work.tile([P, C], U32, align_bytes=64, name=label + "_codes")
+            scales = work.tile([P, C], U8, align_bytes=64, name=label + "_scales")
+            nc.vector.quantize_mx(
+                out=codes[:].bitcast(FP8X4),
+                scales=scales[:],
+                in_=grouped[:].rearrange("p r t -> p (r t)"),
+            )
+            return codes, scales
+
+        def spread_row_factors(b):
+            r_col = work.tile([P, BLOCKS], F32)
+            nc.vector.reciprocal(out=r_col[:], in_=live[b]["row_sum"][:])
+            nc.vector.tensor_scalar_mul(out=r_col[:], in0=r_col[:], scalar1=gamma_col[:, 0:1])
+            r_ps = psum_tr.tile([P, N], F32, tag="tr")
+            for mb in range(BLOCKS):
+                nc.tensor.matmul(
+                    out=r_ps[:, block(mb)],
+                    lhsT=r_col[:, mb : mb + 1].to_broadcast([P, P]),
+                    rhs=ident_f32[:],
+                    start=True,
+                    stop=True,
+                )
+            r_all = work.tile([P, N], F32)
+            nc.scalar.copy(out=r_all[:], in_=r_ps[:])
+            live[b]["r_all"] = r_all
+
+        def attend(b, cb):
+            att_ps = psum_mm.tile([P, N], F32, tag="mm")
+            nc.tensor.matmul_mx(
+                out=att_ps[:],
+                lhsT=live[b]["val_codes"][:, block(cb)].bitcast(FP8X4),
+                lhsT_scale=live[b]["val_scales"][:, block(cb)],
+                rhs=live[b]["e_codes"][:].bitcast(FP8X4),
+                rhs_scale=live[b]["e_scales"][:],
+                start=True,
+                stop=True,
+            )
+            scaled = results.tile([P, N], F32)
+            nc.vector.tensor_tensor(out=scaled[:], in0=att_ps[:], in1=live[b]["r_all"][:], op=ALU.mult)
+            o_sb = results.tile([P, N], F32)
+            nc.gpsimd.tensor_tensor(out=o_sb[:], in0=scaled[:], in1=live[b]["x"][:, cb, :], op=ALU.add)
+            nc.sync.dma_start(out=out[b, block(cb), :], in_=o_sb[:])
+
+        for b in range(PREFETCH):
+            load(b)
+        for step in range(B + 2):
+            first, second, third = step, step - 1, step - 2
+            if first + PREFETCH < B:
+                load(first + PREFETCH)
+            if first < B:
+                transpose_queries(first)
+                quantise_out1(first)
+                begin_scores_and_values(first)
+            if 0 <= second < B:
+                e_grouped = keys_to_partitions(live[second]["e"], "e")
+                val_grouped = keys_to_partitions(live[second]["val"], "val")
+                spread_row_factors(second)
+                live[second]["e_codes"], live[second]["e_scales"] = quantise_along_keys(e_grouped, "e")
+                live[second]["val_codes"], live[second]["val_scales"] = quantise_along_keys(
+                    val_grouped, "val"
+                )
+            for i in range(BLOCKS):
+                if first < B:
+                    scores(first, i)
+                if third >= 0:
+                    attend(third, i)
+                if first < B:
+                    values(first, i)

@@ -19,15 +19,39 @@ N = 512
 D = 128
 P = 128
 PACK = 4
-BLOCKS = C // P
 PAIR = 2
-PREFETCH = 2
+BLOCKS = C // P
+HALF = C // 2
+ALL_BLOCKS = B * BLOCKS
+ALL_HALVES = B * 2
 
 FLOPS = 2 * B * (C * C * N + N * D * N + C * N * N)
+
+LOAD_AHEAD = 14
+QUERIES_AHEAD = 4
+TRANSPOSE = 4
+SPREAD = 7
+ATTEND = 10
+REGROUP_AHEAD = 5
+QUANTISE_OUT1_AHEAD = 4
+QUANTISE_KEYS = 3
+ROW_FACTORS = 2
 
 
 def block(i):
     return slice(i * P, (i + 1) * P)
+
+
+def half(h):
+    return slice(h * HALF, (h + 1) * HALF)
+
+
+def is_block(t):
+    return 0 <= t < ALL_BLOCKS
+
+
+def starts_item(t):
+    return is_block(t) and t % BLOCKS == 0
 
 
 def tile_mvpam_module_mask_cascade_pb_t_kernel(
@@ -36,9 +60,9 @@ def tile_mvpam_module_mask_cascade_pb_t_kernel(
     nc = tc.nc
     with ExitStack() as ctx:
         const = ctx.enter_context(tc.tile_pool(name="const", bufs=1))
-        loads = ctx.enter_context(tc.tile_pool(name="loads", bufs=PREFETCH + 1))
-        residual = ctx.enter_context(tc.tile_pool(name="residual", bufs=PREFETCH + 3))
-        work = ctx.enter_context(tc.tile_pool(name="work", bufs=2))
+        loads = ctx.enter_context(tc.tile_pool(name="loads", bufs=4))
+        long_loads = ctx.enter_context(tc.tile_pool(name="long_loads", bufs=6))
+        work = ctx.enter_context(tc.tile_pool(name="work", bufs=4))
         results = ctx.enter_context(tc.tile_pool(name="results", bufs=4))
         psum_mm = ctx.enter_context(tc.psum_pool(name="psum_mm", bufs=5))
         psum_tr = ctx.enter_context(tc.psum_pool(name="psum_tr", bufs=3))
@@ -75,71 +99,91 @@ def tile_mvpam_module_mask_cascade_pb_t_kernel(
         nc.vector.tensor_copy(out=gamma_col[:], in_=gamma_bf16[:])
 
         live = {}
+        for b in range(B):
+            live[b] = {}
+        banks = {}
 
-        def load(b):
-            q_sb = loads.tile([P, BLOCKS, D], BF16)
+        def item_tile(pool, b, name, shape, dtype):
+            if name not in live[b]:
+                live[b][name] = pool.tile(shape, dtype, name=name, align_bytes=64)
+            return live[b][name]
+
+        def load_front(b):
+            q_sb = item_tile(loads, b, "q_sb", [P, BLOCKS, D], BF16)
             nc.sync.dma_start(out=q_sb[:], in_=q[b].rearrange("(mb p) d -> p mb d", p=P))
-            k_sb = loads.tile([D, N], BF16)
+            k_sb = item_tile(long_loads, b, "k_sb", [D, N], BF16)
             nc.sync.dma_start(out=k_sb[:], in_=k[b])
-            o1_raw = loads.tile([P, PACK, N], BF16)
+            o1_raw = item_tile(loads, b, "o1_raw", [P, PACK, N], BF16)
             nc.sync.dma_start(out=o1_raw[:], in_=out1[b].rearrange("(p j) n -> p j n", j=PACK))
-            x_sb = residual.tile([P, BLOCKS, N], BF16)
+
+        def load_residual(b):
+            x_sb = item_tile(long_loads, b, "x_sb", [P, BLOCKS, N], BF16)
             nc.sync.dma_start(out=x_sb[:], in_=x[b].rearrange("(cb p) m -> p cb m", p=P))
-            live[b] = {"q": q_sb, "k": k_sb, "o1": o1_raw, "x": x_sb}
 
         def transpose_queries(b):
             qT_ps = psum_tr.tile([D, N], BF16, tag="tr")
             for mb in range(BLOCKS):
                 nc.tensor.transpose(
-                    out=qT_ps[:, block(mb)], in_=live[b]["q"][:, mb, :], identity=ident_bf16[:]
+                    out=qT_ps[:, block(mb)], in_=live[b]["q_sb"][:, mb, :], identity=ident_bf16[:]
                 )
-            qT_sb = work.tile([D, N], BF16)
-            nc.scalar.copy(out=qT_sb[:], in_=qT_ps[:])
-            live[b]["qT"] = qT_sb
+            banks["qT", b] = qT_ps
 
-        def quantise_out1(b):
-            o1_grouped = work.tile([P, N, PACK], BF16, align_bytes=64)
-            nc.vector.tensor_copy(
-                out=o1_grouped[:].rearrange("p (c i) j -> p c j i", i=4),
-                in_=live[b]["o1"][:].rearrange("p j (c i) -> p c j i", i=4),
-            )
-            o1_codes = work.tile([P, N], U32, align_bytes=64)
-            o1_scales = work.tile([P, N], U8, align_bytes=64)
-            nc.vector.quantize_mx(
-                out=o1_codes[:].bitcast(FP8X4),
-                scales=o1_scales[:],
-                in_=o1_grouped[:].rearrange("p n j -> p (n j)"),
-            )
-            live[b]["o1_codes"] = o1_codes
-            live[b]["o1_scales"] = o1_scales
+        def copy_queries(b):
+            qT_sb = item_tile(work, b, "qT_sb", [D, N], BF16)
+            nc.scalar.copy(out=qT_sb[:], in_=banks["qT", b][:])
 
-        def begin_scores_and_values(b):
-            live[b]["neg_max"] = work.tile([P, BLOCKS], F32, name="neg_max")
-            live[b]["row_sum"] = work.tile([P, BLOCKS], F32, name="row_sum")
-            live[b]["e"] = work.tile([P, BLOCKS, N], BF16, name="e_sb")
-            live[b]["val"] = work.tile([P, BLOCKS, N], BF16, name="val_sb")
-
-        def scores(b, mb):
-            neg_max = live[b]["neg_max"][:, mb : mb + 1]
+        def scores_matmul(t):
+            b, mb = divmod(t, BLOCKS)
             s_ps = psum_mm.tile([P, N], F32, tag="mm")
             nc.tensor.matmul(
                 out=s_ps[:],
-                lhsT=live[b]["qT"][:, block(mb)],
-                rhs=live[b]["k"][:],
+                lhsT=live[b]["qT_sb"][:, block(mb)],
+                rhs=live[b]["k_sb"][:],
                 start=True,
                 stop=True,
             )
-            nc.vector.tensor_reduce(out=neg_max, in_=s_ps[:], axis=AXIS.X, op=ALU.max, negate=True)
-            nc.scalar.activation(
-                out=live[b]["e"][:, mb, :],
-                in_=s_ps[:],
-                func=ACT.Exp,
-                bias=neg_max,
-                scale=1.0,
-                accum_out=live[b]["row_sum"][:, mb : mb + 1],
+            banks["s", t] = s_ps
+
+        def row_maximum(t):
+            b, mb = divmod(t, BLOCKS)
+            neg_max = item_tile(work, b, "neg_max", [P, BLOCKS], F32)
+            nc.vector.tensor_reduce(
+                out=neg_max[:, mb : mb + 1], in_=banks["s", t][:], axis=AXIS.X, op=ALU.max, negate=True
             )
 
-        def values(b, cb):
+        def exponentials(t):
+            b, mb = divmod(t, BLOCKS)
+            e_sb = item_tile(work, b, "e_sb", [P, BLOCKS, N], BF16)
+            row_sum = item_tile(work, b, "row_sum", [P, BLOCKS], F32)
+            nc.scalar.activation(
+                out=e_sb[:, mb, :],
+                in_=banks["s", t][:],
+                func=ACT.Exp,
+                bias=live[b]["neg_max"][:, mb : mb + 1],
+                scale=1.0,
+                accum_out=row_sum[:, mb : mb + 1],
+            )
+
+        def regroup_out1(g):
+            b, h = divmod(g, 2)
+            o1_grouped = item_tile(work, b, "o1_grouped", [P, N, PACK], BF16)
+            nc.vector.tensor_copy(
+                out=o1_grouped[:, half(h), :].rearrange("p (c i) j -> p c j i", i=4),
+                in_=live[b]["o1_raw"][:, :, half(h)].rearrange("p j (c i) -> p c j i", i=4),
+            )
+
+        def quantise_out1(g):
+            b, h = divmod(g, 2)
+            o1_codes = item_tile(work, b, "o1_codes", [P, N], U32)
+            o1_scales = item_tile(work, b, "o1_scales", [P, N], U8)
+            nc.vector.quantize_mx(
+                out=o1_codes[:, half(h)].bitcast(FP8X4),
+                scales=o1_scales[:, half(h)],
+                in_=live[b]["o1_grouped"][:, half(h), :].rearrange("p n j -> p (n j)"),
+            )
+
+        def values_matmul(t):
+            b, cb = divmod(t, BLOCKS)
             val_ps = psum_mm.tile([P, N], F32, tag="mm")
             nc.tensor.matmul_mx(
                 out=val_ps[:],
@@ -150,66 +194,81 @@ def tile_mvpam_module_mask_cascade_pb_t_kernel(
                 start=True,
                 stop=True,
             )
+            banks["val", t] = val_ps
+
+        def add_bias(t):
+            b, cb = divmod(t, BLOCKS)
+            val_sb = item_tile(work, b, "val_sb", [P, BLOCKS, N], BF16)
             nc.scalar.activation(
-                out=live[b]["val"][:, cb, :],
-                in_=val_ps[:],
+                out=val_sb[:, cb, :],
+                in_=banks["val", t][:],
                 func=ACT.Identity,
                 bias=bias_col[:, cb : cb + 1],
                 scale=1.0,
             )
 
-        def keys_to_partitions(rows_sb, label):
-            grouped = work.tile([P, C, PACK], BF16, align_bytes=64, name=label + "_grouped")
+        def matrix_and_half(t):
+            b, i = divmod(t, BLOCKS)
+            return b, ("e", "val")[i % 2], i // 2
+
+        def transpose_words(t):
+            b, matrix, h = matrix_and_half(t)
+            words_ps = psum_tr.tile([P, 2, PAIR, P], F32, tag="tr")
+            for i in range(2):
+                row_words = live[b][matrix + "_sb"][:, 2 * h + i, :].bitcast(F32)
+                for u in range(PAIR):
+                    nc.tensor.transpose(
+                        out=words_ps[:, i, u, :], in_=row_words[:, block(u)], identity=ident_f32[:]
+                    )
+            banks["words", t] = words_ps
+
+        def copy_words(t):
+            b, matrix, h = matrix_and_half(t)
+            grouped = item_tile(work, b, matrix + "_grouped", [P, C, PACK], BF16)
             grouped_words = (
-                grouped[:]
+                grouped[:, half(h), :]
                 .rearrange("p r t -> p (r t)")
                 .bitcast(F32)
-                .rearrange("p (r u) -> p r u", u=PAIR)
+                .rearrange("p (i r u) -> p i r u", i=2, u=PAIR)
             )
-            for half in range(BLOCKS // 2):
-                words_ps = psum_tr.tile([P, 2, PAIR, P], F32, tag="tr")
-                for i in range(2):
-                    row_words = rows_sb[:, 2 * half + i, :].bitcast(F32)
-                    for u in range(PAIR):
-                        nc.tensor.transpose(
-                            out=words_ps[:, i, u, :], in_=row_words[:, block(u)], identity=ident_f32[:]
-                        )
-                nc.scalar.copy(
-                    out=grouped_words[:, 2 * half * P : (2 * half + 2) * P, :].rearrange(
-                        "p (i r) u -> p i r u", i=2
-                    ),
-                    in_=words_ps[:].rearrange("p i u r -> p i r u"),
-                )
-            return grouped
+            nc.scalar.copy(out=grouped_words, in_=banks["words", t][:].rearrange("p i u r -> p i r u"))
 
-        def quantise_along_keys(grouped, label):
-            codes = work.tile([P, C], U32, align_bytes=64, name=label + "_codes")
-            scales = work.tile([P, C], U8, align_bytes=64, name=label + "_scales")
-            nc.vector.quantize_mx(
-                out=codes[:].bitcast(FP8X4),
-                scales=scales[:],
-                in_=grouped[:].rearrange("p r t -> p (r t)"),
+        def quantise_along_keys(g):
+            b, h = divmod(g, 2)
+            for matrix in ("e", "val"):
+                codes = item_tile(work, b, matrix + "_codes", [P, C], U32)
+                scales = item_tile(work, b, matrix + "_scales", [P, C], U8)
+                nc.vector.quantize_mx(
+                    out=codes[:, half(h)].bitcast(FP8X4),
+                    scales=scales[:, half(h)],
+                    in_=live[b][matrix + "_grouped"][:, half(h), :].rearrange("p r t -> p (r t)"),
+                )
+
+        def row_factors(b):
+            inverse = item_tile(work, b, "inverse", [P, BLOCKS], F32)
+            nc.vector.reciprocal(out=inverse[:], in_=live[b]["row_sum"][:])
+            r_rows = item_tile(work, b, "r_rows", [P, BLOCKS, P], F32)
+            nc.gpsimd.tensor_tensor(
+                out=r_rows[:],
+                in0=inverse[:].unsqueeze(2).to_broadcast([P, BLOCKS, P]),
+                in1=gamma_col[:].unsqueeze(2).to_broadcast([P, BLOCKS, P]),
+                op=ALU.mult,
             )
-            return codes, scales
 
         def spread_row_factors(b):
-            r_col = work.tile([P, BLOCKS], F32)
-            nc.vector.reciprocal(out=r_col[:], in_=live[b]["row_sum"][:])
-            nc.vector.tensor_scalar_mul(out=r_col[:], in0=r_col[:], scalar1=gamma_col[:, 0:1])
             r_ps = psum_tr.tile([P, N], F32, tag="tr")
             for mb in range(BLOCKS):
-                nc.tensor.matmul(
-                    out=r_ps[:, block(mb)],
-                    lhsT=r_col[:, mb : mb + 1].to_broadcast([P, P]),
-                    rhs=ident_f32[:],
-                    start=True,
-                    stop=True,
+                nc.tensor.transpose(
+                    out=r_ps[:, block(mb)], in_=live[b]["r_rows"][:, mb, :], identity=ident_f32[:]
                 )
-            r_all = work.tile([P, N], F32)
-            nc.scalar.copy(out=r_all[:], in_=r_ps[:])
-            live[b]["r_all"] = r_all
+            banks["r", b] = r_ps
 
-        def attend(b, cb):
+        def copy_row_factors(b):
+            r_all = item_tile(work, b, "r_all", [P, N], F32)
+            nc.scalar.copy(out=r_all[:], in_=banks["r", b][:])
+
+        def attend_matmul(t):
+            b, cb = divmod(t, BLOCKS)
             att_ps = psum_mm.tile([P, N], F32, tag="mm")
             nc.tensor.matmul_mx(
                 out=att_ps[:],
@@ -220,34 +279,64 @@ def tile_mvpam_module_mask_cascade_pb_t_kernel(
                 start=True,
                 stop=True,
             )
+            banks["att", t] = att_ps
+
+        def finish(t):
+            b, cb = divmod(t, BLOCKS)
             scaled = results.tile([P, N], F32)
-            nc.vector.tensor_tensor(out=scaled[:], in0=att_ps[:], in1=live[b]["r_all"][:], op=ALU.mult)
+            nc.vector.tensor_tensor(
+                out=scaled[:], in0=banks["att", t][:], in1=live[b]["r_all"][:], op=ALU.mult
+            )
             o_sb = results.tile([P, N], F32)
-            nc.gpsimd.tensor_tensor(out=o_sb[:], in0=scaled[:], in1=live[b]["x"][:, cb, :], op=ALU.add)
+            nc.gpsimd.tensor_tensor(
+                out=o_sb[:], in0=scaled[:], in1=live[b]["x_sb"][:, cb, :], op=ALU.add
+            )
             nc.sync.dma_start(out=out[b, block(cb), :], in_=o_sb[:])
 
-        for b in range(PREFETCH):
-            load(b)
-        for step in range(B + 2):
-            first, second, third = step, step - 1, step - 2
-            if first + PREFETCH < B:
-                load(first + PREFETCH)
-            if first < B:
-                transpose_queries(first)
-                quantise_out1(first)
-                begin_scores_and_values(first)
-            if 0 <= second < B:
-                e_grouped = keys_to_partitions(live[second]["e"], "e")
-                val_grouped = keys_to_partitions(live[second]["val"], "val")
-                spread_row_factors(second)
-                live[second]["e_codes"], live[second]["e_scales"] = quantise_along_keys(e_grouped, "e")
-                live[second]["val_codes"], live[second]["val_scales"] = quantise_along_keys(
-                    val_grouped, "val"
-                )
-            for i in range(BLOCKS):
-                if first < B:
-                    scores(first, i)
-                if third >= 0:
-                    attend(third, i)
-                if first < B:
-                    values(first, i)
+        def one_slot(slot):
+            if starts_item(slot + LOAD_AHEAD):
+                load_front((slot + LOAD_AHEAD) // BLOCKS)
+            if starts_item(slot):
+                load_residual(slot // BLOCKS)
+            if is_block(slot - 1 - ATTEND):
+                finish(slot - 1 - ATTEND)
+            if is_block(slot - 1):
+                exponentials(slot - 1)
+            if is_block(slot - 1 - TRANSPOSE):
+                copy_words(slot - 1 - TRANSPOSE)
+            if is_block(slot - 1):
+                add_bias(slot - 1)
+            if starts_item(slot - 1 - SPREAD):
+                copy_row_factors((slot - 1 - SPREAD) // BLOCKS)
+            if starts_item(slot - 1 + QUERIES_AHEAD):
+                copy_queries((slot - 1 + QUERIES_AHEAD) // BLOCKS)
+            if is_block(slot):
+                scores_matmul(slot)
+            if is_block(slot - ATTEND):
+                attend_matmul(slot - ATTEND)
+            if is_block(slot):
+                values_matmul(slot)
+            if is_block(slot - TRANSPOSE):
+                transpose_words(slot - TRANSPOSE)
+            if starts_item(slot - SPREAD):
+                spread_row_factors((slot - SPREAD) // BLOCKS)
+            if starts_item(slot + QUERIES_AHEAD):
+                transpose_queries((slot + QUERIES_AHEAD) // BLOCKS)
+            if is_block(slot):
+                row_maximum(slot)
+
+        def vector_work_on_sbuf(pair):
+            if 0 <= pair - ROW_FACTORS < ALL_HALVES and (pair - ROW_FACTORS) % 2 == 0:
+                row_factors((pair - ROW_FACTORS) // 2)
+            if 0 <= pair - QUANTISE_KEYS < ALL_HALVES:
+                quantise_along_keys(pair - QUANTISE_KEYS)
+            if 0 <= pair + QUANTISE_OUT1_AHEAD < ALL_HALVES:
+                quantise_out1(pair + QUANTISE_OUT1_AHEAD)
+            if 0 <= pair + REGROUP_AHEAD < ALL_HALVES:
+                regroup_out1(pair + REGROUP_AHEAD)
+
+        with tc.manual_schedule():
+            for pair in range(-LOAD_AHEAD // 2, (ALL_BLOCKS + ATTEND + 2) // 2):
+                one_slot(2 * pair)
+                one_slot(2 * pair + 1)
+                vector_work_on_sbuf(pair)

@@ -23,19 +23,19 @@ PAIR = 2
 BLOCKS = C // P
 HALF = C // 2
 ALL_BLOCKS = B * BLOCKS
-ALL_HALVES = B * 2
 
 FLOPS = 2 * B * (C * C * N + N * D * N + C * N * N)
 
-LOAD_AHEAD = 14
+LOAD_AHEAD = 12
+REGROUP_AHEAD = 8
+QUANTISE_OUT1_AHEAD = 6
 QUERIES_AHEAD = 4
 TRANSPOSE = 4
-SPREAD = 7
+LOAD_RESIDUAL = 4
+ROW_FACTORS = 5
+QUANTISE_KEYS = 6
 ATTEND = 10
-REGROUP_AHEAD = 5
-QUANTISE_OUT1_AHEAD = 4
-QUANTISE_KEYS = 3
-ROW_FACTORS = 2
+BACK = 15
 
 
 def block(i):
@@ -61,8 +61,7 @@ def tile_mvpam_module_mask_cascade_pb_t_kernel(
     with ExitStack() as ctx:
         const = ctx.enter_context(tc.tile_pool(name="const", bufs=1))
         loads = ctx.enter_context(tc.tile_pool(name="loads", bufs=4))
-        long_loads = ctx.enter_context(tc.tile_pool(name="long_loads", bufs=6))
-        work = ctx.enter_context(tc.tile_pool(name="work", bufs=4))
+        work = ctx.enter_context(tc.tile_pool(name="work", bufs=3))
         results = ctx.enter_context(tc.tile_pool(name="results", bufs=4))
         psum_mm = ctx.enter_context(tc.psum_pool(name="psum_mm", bufs=5))
         psum_tr = ctx.enter_context(tc.psum_pool(name="psum_tr", bufs=3))
@@ -111,13 +110,13 @@ def tile_mvpam_module_mask_cascade_pb_t_kernel(
         def load_front(b):
             q_sb = item_tile(loads, b, "q_sb", [P, BLOCKS, D], BF16)
             nc.sync.dma_start(out=q_sb[:], in_=q[b].rearrange("(mb p) d -> p mb d", p=P))
-            k_sb = item_tile(long_loads, b, "k_sb", [D, N], BF16)
+            k_sb = item_tile(loads, b, "k_sb", [D, N], BF16)
             nc.sync.dma_start(out=k_sb[:], in_=k[b])
             o1_raw = item_tile(loads, b, "o1_raw", [P, PACK, N], BF16)
             nc.sync.dma_start(out=o1_raw[:], in_=out1[b].rearrange("(p j) n -> p j n", j=PACK))
 
         def load_residual(b):
-            x_sb = item_tile(long_loads, b, "x_sb", [P, BLOCKS, N], BF16)
+            x_sb = item_tile(loads, b, "x_sb", [P, BLOCKS, N], BF16)
             nc.sync.dma_start(out=x_sb[:], in_=x[b].rearrange("(cb p) m -> p cb m", p=P))
 
         def transpose_queries(b):
@@ -164,22 +163,22 @@ def tile_mvpam_module_mask_cascade_pb_t_kernel(
                 accum_out=row_sum[:, mb : mb + 1],
             )
 
-        def regroup_out1(g):
-            b, h = divmod(g, 2)
+        def regroup_out1(t):
+            b, nb = divmod(t, BLOCKS)
             o1_grouped = item_tile(work, b, "o1_grouped", [P, N, PACK], BF16)
             nc.vector.tensor_copy(
-                out=o1_grouped[:, half(h), :].rearrange("p (c i) j -> p c j i", i=4),
-                in_=live[b]["o1_raw"][:, :, half(h)].rearrange("p j (c i) -> p c j i", i=4),
+                out=o1_grouped[:, block(nb), :].rearrange("p (c i) j -> p c j i", i=4),
+                in_=live[b]["o1_raw"][:, :, block(nb)].rearrange("p j (c i) -> p c j i", i=4),
             )
 
-        def quantise_out1(g):
-            b, h = divmod(g, 2)
+        def quantise_out1(t):
+            b, nb = divmod(t, BLOCKS)
             o1_codes = item_tile(work, b, "o1_codes", [P, N], U32)
             o1_scales = item_tile(work, b, "o1_scales", [P, N], U8)
             nc.vector.quantize_mx(
-                out=o1_codes[:, half(h)].bitcast(FP8X4),
-                scales=o1_scales[:, half(h)],
-                in_=live[b]["o1_grouped"][:, half(h), :].rearrange("p n j -> p (n j)"),
+                out=o1_codes[:, block(nb)].bitcast(FP8X4),
+                scales=o1_scales[:, block(nb)],
+                in_=live[b]["o1_grouped"][:, block(nb), :].rearrange("p n j -> p (n j)"),
             )
 
         def values_matmul(t):
@@ -231,83 +230,83 @@ def tile_mvpam_module_mask_cascade_pb_t_kernel(
                 .bitcast(F32)
                 .rearrange("p (i r u) -> p i r u", i=2, u=PAIR)
             )
-            nc.scalar.copy(out=grouped_words, in_=banks["words", t][:].rearrange("p i u r -> p i r u"))
+            words = banks["words", t][:].rearrange("p i u r -> p i r u")
+            if matrix == "e":
+                nc.scalar.copy(out=grouped_words, in_=words)
+            else:
+                nc.vector.tensor_copy(out=grouped_words, in_=words)
 
-        def quantise_along_keys(g):
-            b, h = divmod(g, 2)
-            for matrix in ("e", "val"):
-                codes = item_tile(work, b, matrix + "_codes", [P, C], U32)
-                scales = item_tile(work, b, matrix + "_scales", [P, C], U8)
-                nc.vector.quantize_mx(
-                    out=codes[:, half(h)].bitcast(FP8X4),
-                    scales=scales[:, half(h)],
-                    in_=live[b][matrix + "_grouped"][:, half(h), :].rearrange("p r t -> p (r t)"),
-                )
-
-        def row_factors(b):
-            inverse = item_tile(work, b, "inverse", [P, BLOCKS], F32)
-            nc.vector.reciprocal(out=inverse[:], in_=live[b]["row_sum"][:])
-            r_rows = item_tile(work, b, "r_rows", [P, BLOCKS, P], F32)
-            nc.gpsimd.tensor_tensor(
-                out=r_rows[:],
-                in0=inverse[:].unsqueeze(2).to_broadcast([P, BLOCKS, P]),
-                in1=gamma_col[:].unsqueeze(2).to_broadcast([P, BLOCKS, P]),
-                op=ALU.mult,
+        def quantise_along_keys(t):
+            b, matrix, h = matrix_and_half(t)
+            codes = item_tile(work, b, matrix + "_codes", [P, C], U32)
+            scales = item_tile(work, b, matrix + "_scales", [P, C], U8)
+            nc.vector.quantize_mx(
+                out=codes[:, half(h)].bitcast(FP8X4),
+                scales=scales[:, half(h)],
+                in_=live[b][matrix + "_grouped"][:, half(h), :].rearrange("p r t -> p (r t)"),
             )
 
-        def spread_row_factors(b):
-            r_ps = psum_tr.tile([P, N], F32, tag="tr")
-            for mb in range(BLOCKS):
-                nc.tensor.transpose(
-                    out=r_ps[:, block(mb)], in_=live[b]["r_rows"][:, mb, :], identity=ident_f32[:]
-                )
-            banks["r", b] = r_ps
-
-        def copy_row_factors(b):
-            r_all = item_tile(work, b, "r_all", [P, N], F32)
-            nc.scalar.copy(out=r_all[:], in_=banks["r", b][:])
+        def row_factors(b):
+            r_col = item_tile(work, b, "r_col", [P, BLOCKS], F32)
+            nc.vector.reciprocal(out=r_col[:], in_=live[b]["row_sum"][:])
+            nc.vector.tensor_scalar_mul(out=r_col[:], in0=r_col[:], scalar1=gamma_col[:, 0:1])
 
         def attend_matmul(t):
-            b, cb = divmod(t, BLOCKS)
-            att_ps = psum_mm.tile([P, N], F32, tag="mm")
+            b, mb = divmod(t, BLOCKS)
+            att_ps = psum_mm.tile([P, C], F32, tag="mm")
             nc.tensor.matmul_mx(
                 out=att_ps[:],
-                lhsT=live[b]["val_codes"][:, block(cb)].bitcast(FP8X4),
-                lhsT_scale=live[b]["val_scales"][:, block(cb)],
-                rhs=live[b]["e_codes"][:].bitcast(FP8X4),
-                rhs_scale=live[b]["e_scales"][:],
+                lhsT=live[b]["e_codes"][:, block(mb)].bitcast(FP8X4),
+                lhsT_scale=live[b]["e_scales"][:, block(mb)],
+                rhs=live[b]["val_codes"][:].bitcast(FP8X4),
+                rhs_scale=live[b]["val_scales"][:],
                 start=True,
                 stop=True,
             )
             banks["att", t] = att_ps
 
-        def finish(t):
-            b, cb = divmod(t, BLOCKS)
-            scaled = results.tile([P, N], F32)
-            nc.vector.tensor_tensor(
-                out=scaled[:], in0=banks["att", t][:], in1=live[b]["r_all"][:], op=ALU.mult
+        def scale_rows(t):
+            b, mb = divmod(t, BLOCKS)
+            scaled = item_tile(work, b, "scaled", [P, BLOCKS, C], F32)
+            nc.scalar.activation(
+                out=scaled[:, mb, :],
+                in_=banks["att", t][:],
+                func=ACT.Copy,
+                scale=live[b]["r_col"][:, mb : mb + 1],
             )
+
+        def transpose_back(t):
+            b, cb = divmod(t, BLOCKS)
+            o_ps = psum_tr.tile([P, N], F32, tag="tr")
+            for mb in range(BLOCKS):
+                nc.tensor.transpose(
+                    out=o_ps[:, block(mb)], in_=live[b]["scaled"][:, mb, block(cb)], identity=ident_f32[:]
+                )
+            banks["o", t] = o_ps
+
+        def add_residual(t):
+            b, cb = divmod(t, BLOCKS)
             o_sb = results.tile([P, N], F32)
-            nc.gpsimd.tensor_tensor(
-                out=o_sb[:], in0=scaled[:], in1=live[b]["x_sb"][:, cb, :], op=ALU.add
+            nc.vector.tensor_tensor(
+                out=o_sb[:], in0=banks["o", t][:], in1=live[b]["x_sb"][:, cb, :], op=ALU.add
             )
             nc.sync.dma_start(out=out[b, block(cb), :], in_=o_sb[:])
 
         def one_slot(slot):
             if starts_item(slot + LOAD_AHEAD):
                 load_front((slot + LOAD_AHEAD) // BLOCKS)
-            if starts_item(slot):
-                load_residual(slot // BLOCKS)
-            if is_block(slot - 1 - ATTEND):
-                finish(slot - 1 - ATTEND)
+            if starts_item(slot - LOAD_RESIDUAL):
+                load_residual((slot - LOAD_RESIDUAL) // BLOCKS)
+            if is_block(slot - 1 - BACK):
+                add_residual(slot - 1 - BACK)
             if is_block(slot - 1):
                 exponentials(slot - 1)
             if is_block(slot - 1 - TRANSPOSE):
                 copy_words(slot - 1 - TRANSPOSE)
             if is_block(slot - 1):
                 add_bias(slot - 1)
-            if starts_item(slot - 1 - SPREAD):
-                copy_row_factors((slot - 1 - SPREAD) // BLOCKS)
+            if is_block(slot - 1 - ATTEND):
+                scale_rows(slot - 1 - ATTEND)
             if starts_item(slot - 1 + QUERIES_AHEAD):
                 copy_queries((slot - 1 + QUERIES_AHEAD) // BLOCKS)
             if is_block(slot):
@@ -318,25 +317,21 @@ def tile_mvpam_module_mask_cascade_pb_t_kernel(
                 values_matmul(slot)
             if is_block(slot - TRANSPOSE):
                 transpose_words(slot - TRANSPOSE)
-            if starts_item(slot - SPREAD):
-                spread_row_factors((slot - SPREAD) // BLOCKS)
+            if is_block(slot - BACK):
+                transpose_back(slot - BACK)
             if starts_item(slot + QUERIES_AHEAD):
                 transpose_queries((slot + QUERIES_AHEAD) // BLOCKS)
             if is_block(slot):
                 row_maximum(slot)
-
-        def vector_work_on_sbuf(pair):
-            if 0 <= pair - ROW_FACTORS < ALL_HALVES and (pair - ROW_FACTORS) % 2 == 0:
-                row_factors((pair - ROW_FACTORS) // 2)
-            if 0 <= pair - QUANTISE_KEYS < ALL_HALVES:
-                quantise_along_keys(pair - QUANTISE_KEYS)
-            if 0 <= pair + QUANTISE_OUT1_AHEAD < ALL_HALVES:
-                quantise_out1(pair + QUANTISE_OUT1_AHEAD)
-            if 0 <= pair + REGROUP_AHEAD < ALL_HALVES:
-                regroup_out1(pair + REGROUP_AHEAD)
+            if starts_item(slot - ROW_FACTORS):
+                row_factors((slot - ROW_FACTORS) // BLOCKS)
+            if is_block(slot - QUANTISE_KEYS):
+                quantise_along_keys(slot - QUANTISE_KEYS)
+            if is_block(slot + QUANTISE_OUT1_AHEAD):
+                quantise_out1(slot + QUANTISE_OUT1_AHEAD)
+            if is_block(slot + REGROUP_AHEAD):
+                regroup_out1(slot + REGROUP_AHEAD)
 
         with tc.manual_schedule():
-            for pair in range(-LOAD_AHEAD // 2, (ALL_BLOCKS + ATTEND + 2) // 2):
-                one_slot(2 * pair)
-                one_slot(2 * pair + 1)
-                vector_work_on_sbuf(pair)
+            for slot in range(-LOAD_AHEAD, ALL_BLOCKS + BACK + 1):
+                one_slot(slot)

@@ -63,8 +63,7 @@ def tile_mvpam_module_mask_cascade_pb_t_kernel(
         loads = ctx.enter_context(tc.tile_pool(name="loads", bufs=4))
         work = ctx.enter_context(tc.tile_pool(name="work", bufs=3))
         results = ctx.enter_context(tc.tile_pool(name="results", bufs=4))
-        psum_mm = ctx.enter_context(tc.psum_pool(name="psum_mm", bufs=5))
-        psum_tr = ctx.enter_context(tc.psum_pool(name="psum_tr", bufs=3))
+        psum = ctx.enter_context(tc.psum_pool(name="psum", bufs=8))
 
         w_codes = const.tile([P, C], U32, align_bytes=64)
         nc.sync.dma_start(
@@ -87,7 +86,7 @@ def tile_mvpam_module_mask_cascade_pb_t_kernel(
         bias_rows = const.tile([P, P], BF16)
         nc.vector.memset(bias_rows[:], 0.0)
         nc.sync.dma_start(out=bias_rows[0:BLOCKS, :], in_=bv2.rearrange("(cb p) -> cb p", p=P))
-        bias_ps = psum_tr.tile([P, P], BF16, tag="tr")
+        bias_ps = psum.tile([P, P], BF16, tag="bank")
         nc.tensor.transpose(out=bias_ps[:], in_=bias_rows[:], identity=ident_bf16[:])
         bias_col = const.tile([P, BLOCKS], F32)
         nc.vector.tensor_copy(out=bias_col[:], in_=bias_ps[:, 0:BLOCKS])
@@ -120,7 +119,7 @@ def tile_mvpam_module_mask_cascade_pb_t_kernel(
             nc.sync.dma_start(out=x_sb[:], in_=x[b].rearrange("(cb p) m -> p cb m", p=P))
 
         def transpose_queries(b):
-            qT_ps = psum_tr.tile([D, N], BF16, tag="tr")
+            qT_ps = psum.tile([D, N], BF16, tag="bank")
             for mb in range(BLOCKS):
                 nc.tensor.transpose(
                     out=qT_ps[:, block(mb)], in_=live[b]["q_sb"][:, mb, :], identity=ident_bf16[:]
@@ -133,7 +132,7 @@ def tile_mvpam_module_mask_cascade_pb_t_kernel(
 
         def scores_matmul(t):
             b, mb = divmod(t, BLOCKS)
-            s_ps = psum_mm.tile([P, N], F32, tag="mm")
+            s_ps = psum.tile([P, N], F32, tag="bank")
             nc.tensor.matmul(
                 out=s_ps[:],
                 lhsT=live[b]["qT_sb"][:, block(mb)],
@@ -183,7 +182,7 @@ def tile_mvpam_module_mask_cascade_pb_t_kernel(
 
         def values_matmul(t):
             b, cb = divmod(t, BLOCKS)
-            val_ps = psum_mm.tile([P, N], F32, tag="mm")
+            val_ps = psum.tile([P, N], F32, tag="bank")
             nc.tensor.matmul_mx(
                 out=val_ps[:],
                 lhsT=w_codes[:, block(cb)].bitcast(FP8X4),
@@ -212,7 +211,7 @@ def tile_mvpam_module_mask_cascade_pb_t_kernel(
 
         def transpose_words(t):
             b, matrix, h = matrix_and_half(t)
-            words_ps = psum_tr.tile([P, 2, PAIR, P], F32, tag="tr")
+            words_ps = psum.tile([P, 2, PAIR, P], F32, tag="bank")
             for i in range(2):
                 row_words = live[b][matrix + "_sb"][:, 2 * h + i, :].bitcast(F32)
                 for u in range(PAIR):
@@ -253,7 +252,7 @@ def tile_mvpam_module_mask_cascade_pb_t_kernel(
 
         def attend_matmul(t):
             b, mb = divmod(t, BLOCKS)
-            att_ps = psum_mm.tile([P, C], F32, tag="mm")
+            att_ps = psum.tile([P, C], F32, tag="bank")
             nc.tensor.matmul_mx(
                 out=att_ps[:],
                 lhsT=live[b]["e_codes"][:, block(mb)].bitcast(FP8X4),
@@ -277,7 +276,7 @@ def tile_mvpam_module_mask_cascade_pb_t_kernel(
 
         def transpose_back(t):
             b, cb = divmod(t, BLOCKS)
-            o_ps = psum_tr.tile([P, N], F32, tag="tr")
+            o_ps = psum.tile([P, N], F32, tag="bank")
             for mb in range(BLOCKS):
                 nc.tensor.transpose(
                     out=o_ps[:, block(mb)], in_=live[b]["scaled"][:, mb, block(cb)], identity=ident_f32[:]
@@ -297,12 +296,12 @@ def tile_mvpam_module_mask_cascade_pb_t_kernel(
                 load_front((slot + LOAD_AHEAD) // BLOCKS)
             if starts_item(slot - LOAD_RESIDUAL):
                 load_residual((slot - LOAD_RESIDUAL) // BLOCKS)
-            if is_block(slot - 1 - BACK):
-                add_residual(slot - 1 - BACK)
-            if is_block(slot - 1):
-                exponentials(slot - 1)
             if is_block(slot - 1 - TRANSPOSE):
                 copy_words(slot - 1 - TRANSPOSE)
+            if is_block(slot - 1):
+                exponentials(slot - 1)
+            if is_block(slot - 1 - BACK):
+                add_residual(slot - 1 - BACK)
             if is_block(slot - 1):
                 add_bias(slot - 1)
             if is_block(slot - 1 - ATTEND):
@@ -311,16 +310,16 @@ def tile_mvpam_module_mask_cascade_pb_t_kernel(
                 copy_queries((slot - 1 + QUERIES_AHEAD) // BLOCKS)
             if is_block(slot):
                 scores_matmul(slot)
-            if is_block(slot - ATTEND):
-                attend_matmul(slot - ATTEND)
-            if is_block(slot):
-                values_matmul(slot)
             if is_block(slot - TRANSPOSE):
                 transpose_words(slot - TRANSPOSE)
             if is_block(slot - BACK):
                 transpose_back(slot - BACK)
             if starts_item(slot + QUERIES_AHEAD):
                 transpose_queries((slot + QUERIES_AHEAD) // BLOCKS)
+            if is_block(slot):
+                values_matmul(slot)
+            if is_block(slot - ATTEND):
+                attend_matmul(slot - ATTEND)
             if is_block(slot):
                 row_maximum(slot)
             if starts_item(slot - ROW_FACTORS):

@@ -29,13 +29,14 @@ FLOPS = 2 * B * (C * C * N + N * D * N + C * N * N)
 LOAD_AHEAD = 12
 REGROUP_AHEAD = 8
 QUANTISE_OUT1_AHEAD = 6
+REGROUPED_BUFFERS = REGROUP_AHEAD - QUANTISE_OUT1_AHEAD
 QUERIES_AHEAD = 4
 TRANSPOSE = 4
 LOAD_RESIDUAL = 4
 ROW_FACTORS = 5
 QUANTISE_KEYS = 6
 ATTEND = 10
-BACK = 15
+BACK = 12
 
 
 def block(i):
@@ -62,6 +63,7 @@ def tile_mvpam_module_mask_cascade_pb_t_kernel(
         const = ctx.enter_context(tc.tile_pool(name="const", bufs=1))
         loads = ctx.enter_context(tc.tile_pool(name="loads", bufs=4))
         work = ctx.enter_context(tc.tile_pool(name="work", bufs=3))
+        regrouped = ctx.enter_context(tc.tile_pool(name="regrouped", bufs=REGROUPED_BUFFERS))
         results = ctx.enter_context(tc.tile_pool(name="results", bufs=4))
         psum = ctx.enter_context(tc.psum_pool(name="psum", bufs=8))
 
@@ -107,12 +109,12 @@ def tile_mvpam_module_mask_cascade_pb_t_kernel(
             return live[b][name]
 
         def load_front(b):
+            o1_raw = item_tile(loads, b, "o1_raw", [P, PACK, N], BF16)
+            nc.sync.dma_start(out=o1_raw[:], in_=out1[b].rearrange("(p j) n -> p j n", j=PACK))
             q_sb = item_tile(loads, b, "q_sb", [P, BLOCKS, D], BF16)
             nc.sync.dma_start(out=q_sb[:], in_=q[b].rearrange("(mb p) d -> p mb d", p=P))
             k_sb = item_tile(loads, b, "k_sb", [D, N], BF16)
             nc.sync.dma_start(out=k_sb[:], in_=k[b])
-            o1_raw = item_tile(loads, b, "o1_raw", [P, PACK, N], BF16)
-            nc.sync.dma_start(out=o1_raw[:], in_=out1[b].rearrange("(p j) n -> p j n", j=PACK))
 
         def load_residual(b):
             x_sb = item_tile(loads, b, "x_sb", [P, BLOCKS, N], BF16)
@@ -128,7 +130,7 @@ def tile_mvpam_module_mask_cascade_pb_t_kernel(
 
         def copy_queries(b):
             qT_sb = item_tile(work, b, "qT_sb", [D, N], BF16)
-            nc.scalar.copy(out=qT_sb[:], in_=banks["qT", b][:])
+            nc.vector.tensor_copy(out=qT_sb[:], in_=banks["qT", b][:])
 
         def scores_matmul(t):
             b, mb = divmod(t, BLOCKS)
@@ -164,11 +166,16 @@ def tile_mvpam_module_mask_cascade_pb_t_kernel(
 
         def regroup_out1(t):
             b, nb = divmod(t, BLOCKS)
-            o1_grouped = item_tile(work, b, "o1_grouped", [P, N, PACK], BF16)
-            nc.vector.tensor_copy(
-                out=o1_grouped[:, block(nb), :].rearrange("p (c i) j -> p c j i", i=4),
-                in_=live[b]["o1_raw"][:, :, block(nb)].rearrange("p j (c i) -> p c j i", i=4),
+            o1_grouped = regrouped.tile([P, P, PACK], BF16, align_bytes=64)
+            nc.gpsimd.tensor_scalar(
+                out=o1_grouped[:],
+                in0=live[b]["o1_raw"][:, :, block(nb)].rearrange("p j n -> p n j"),
+                scalar1=1.0,
+                scalar2=0.0,
+                op0=ALU.mult,
+                op1=ALU.add,
             )
+            banks["o1_grouped", t] = o1_grouped
 
         def quantise_out1(t):
             b, nb = divmod(t, BLOCKS)
@@ -177,7 +184,7 @@ def tile_mvpam_module_mask_cascade_pb_t_kernel(
             nc.vector.quantize_mx(
                 out=o1_codes[:, block(nb)].bitcast(FP8X4),
                 scales=o1_scales[:, block(nb)],
-                in_=live[b]["o1_grouped"][:, block(nb), :].rearrange("p n j -> p (n j)"),
+                in_=banks["o1_grouped", t][:].rearrange("p n j -> p (n j)"),
             )
 
         def values_matmul(t):
@@ -266,30 +273,32 @@ def tile_mvpam_module_mask_cascade_pb_t_kernel(
 
         def scale_rows(t):
             b, mb = divmod(t, BLOCKS)
-            scaled = item_tile(work, b, "scaled", [P, BLOCKS, C], F32)
+            scaled = results.tile([P, C], F32)
             nc.scalar.activation(
-                out=scaled[:, mb, :],
+                out=scaled[:],
                 in_=banks["att", t][:],
                 func=ACT.Copy,
                 scale=live[b]["r_col"][:, mb : mb + 1],
             )
+            banks["scaled", t] = scaled
 
         def transpose_back(t):
-            b, cb = divmod(t, BLOCKS)
-            o_ps = psum.tile([P, N], F32, tag="bank")
-            for mb in range(BLOCKS):
+            o_ps = psum.tile([P, BLOCKS, P], F32, tag="bank")
+            for cb in range(BLOCKS):
                 nc.tensor.transpose(
-                    out=o_ps[:, block(mb)], in_=live[b]["scaled"][:, mb, block(cb)], identity=ident_f32[:]
+                    out=o_ps[:, cb, :], in_=banks["scaled", t][:, block(cb)], identity=ident_f32[:]
                 )
             banks["o", t] = o_ps
 
         def add_residual(t):
-            b, cb = divmod(t, BLOCKS)
-            o_sb = results.tile([P, N], F32)
+            b, mb = divmod(t, BLOCKS)
+            o_sb = results.tile([P, BLOCKS, P], F32)
             nc.vector.tensor_tensor(
-                out=o_sb[:], in0=banks["o", t][:], in1=live[b]["x_sb"][:, cb, :], op=ALU.add
+                out=o_sb[:], in0=banks["o", t][:], in1=live[b]["x_sb"][:, :, block(mb)], op=ALU.add
             )
-            nc.sync.dma_start(out=out[b, block(cb), :], in_=o_sb[:])
+            nc.sync.dma_start(
+                out=out[b].rearrange("(cb p) m -> p cb m", p=P)[:, :, block(mb)], in_=o_sb[:]
+            )
 
         def one_slot(slot):
             if starts_item(slot + LOAD_AHEAD):

@@ -27,10 +27,11 @@ ALL_BLOCKS = B * BLOCKS
 FLOPS = 2 * B * (C * C * N + N * D * N + C * N * N)
 
 LOAD_AHEAD = 12
-REGROUP_AHEAD = 8
-QUANTISE_OUT1_AHEAD = 6
+QUERIES_AHEAD = 6
+REGROUP_AHEAD = 4
+QUANTISE_OUT1_AHEAD = 2
 REGROUPED_BUFFERS = REGROUP_AHEAD - QUANTISE_OUT1_AHEAD
-QUERIES_AHEAD = 4
+VALUES = 2
 TRANSPOSE = 4
 LOAD_RESIDUAL = 4
 ROW_FACTORS = 5
@@ -109,12 +110,12 @@ def tile_mvpam_module_mask_cascade_pb_t_kernel(
             return live[b][name]
 
         def load_front(b):
-            o1_raw = item_tile(loads, b, "o1_raw", [P, PACK, N], BF16)
-            nc.sync.dma_start(out=o1_raw[:], in_=out1[b].rearrange("(p j) n -> p j n", j=PACK))
             q_sb = item_tile(loads, b, "q_sb", [P, BLOCKS, D], BF16)
             nc.sync.dma_start(out=q_sb[:], in_=q[b].rearrange("(mb p) d -> p mb d", p=P))
             k_sb = item_tile(loads, b, "k_sb", [D, N], BF16)
             nc.sync.dma_start(out=k_sb[:], in_=k[b])
+            o1_raw = item_tile(loads, b, "o1_raw", [P, PACK, N], BF16)
+            nc.sync.dma_start(out=o1_raw[:], in_=out1[b].rearrange("(p j) n -> p j n", j=PACK))
 
         def load_residual(b):
             x_sb = item_tile(loads, b, "x_sb", [P, BLOCKS, N], BF16)
@@ -311,8 +312,8 @@ def tile_mvpam_module_mask_cascade_pb_t_kernel(
                 exponentials(slot - 1)
             if is_block(slot - 1 - BACK):
                 add_residual(slot - 1 - BACK)
-            if is_block(slot - 1):
-                add_bias(slot - 1)
+            if is_block(slot - 1 - VALUES):
+                add_bias(slot - 1 - VALUES)
             if is_block(slot - 1 - ATTEND):
                 scale_rows(slot - 1 - ATTEND)
             if starts_item(slot - 1 + QUERIES_AHEAD):
@@ -325,8 +326,8 @@ def tile_mvpam_module_mask_cascade_pb_t_kernel(
                 transpose_back(slot - BACK)
             if starts_item(slot + QUERIES_AHEAD):
                 transpose_queries((slot + QUERIES_AHEAD) // BLOCKS)
-            if is_block(slot):
-                values_matmul(slot)
+            if is_block(slot - VALUES):
+                values_matmul(slot - VALUES)
             if is_block(slot - ATTEND):
                 attend_matmul(slot - ATTEND)
             if is_block(slot):

@@ -68,36 +68,38 @@ def tile_mvpam_module_mask_cascade_pb_t_kernel(
         results = ctx.enter_context(tc.tile_pool(name="results", bufs=4))
         psum = ctx.enter_context(tc.psum_pool(name="psum", bufs=8))
 
-        w_codes = const.tile([P, C], U32, align_bytes=64)
-        nc.sync.dma_start(
-            out=w_codes[:].bitcast(I32),
-            in_=wv2_words[0].rearrange("p c t -> p (c t)").bitcast(I32),
-        )
-        w_scales = const.tile([P, C], U8, align_bytes=64)
-        nc.vector.memset(w_scales[:].bitcast(I32), 0)
-        for quadrant in range(4):
-            nc.sync.dma_start(
-                out=w_scales[32 * quadrant : 32 * quadrant + 4, :].bitcast(I32),
-                in_=wv2_scales[0, 4 * quadrant : 4 * quadrant + 4, :].bitcast(I32),
-            )
-
         ident_bf16 = const.tile([P, P], BF16)
         make_identity(nc, ident_bf16[:])
         ident_f32 = const.tile([P, P], F32)
         make_identity(nc, ident_f32[:])
 
+        w_codes = const.tile([P, C], U32, align_bytes=64)
+        w_scales = const.tile([P, C], U8, align_bytes=64)
+        nc.vector.memset(w_scales[:].bitcast(I32), 0)
         bias_rows = const.tile([P, P], BF16)
         nc.vector.memset(bias_rows[:], 0.0)
-        nc.sync.dma_start(out=bias_rows[0:BLOCKS, :], in_=bv2.rearrange("(cb p) -> cb p", p=P))
-        bias_ps = psum.tile([P, P], BF16, tag="bank")
-        nc.tensor.transpose(out=bias_ps[:], in_=bias_rows[:], identity=ident_bf16[:])
         bias_col = const.tile([P, BLOCKS], F32)
-        nc.vector.tensor_copy(out=bias_col[:], in_=bias_ps[:, 0:BLOCKS])
-
         gamma_bf16 = const.tile([P, 1], BF16)
-        nc.sync.dma_start(out=gamma_bf16[:], in_=gamma.partition_broadcast(P))
         gamma_col = const.tile([P, 1], F32)
-        nc.vector.tensor_copy(out=gamma_col[:], in_=gamma_bf16[:])
+
+        def load_constants():
+            nc.sync.dma_start(
+                out=w_codes[:].bitcast(I32),
+                in_=wv2_words[0].rearrange("p c t -> p (c t)").bitcast(I32),
+            )
+            for quadrant in range(4):
+                nc.sync.dma_start(
+                    out=w_scales[32 * quadrant : 32 * quadrant + 4, :].bitcast(I32),
+                    in_=wv2_scales[0, 4 * quadrant : 4 * quadrant + 4, :].bitcast(I32),
+                )
+            nc.sync.dma_start(out=bias_rows[0:BLOCKS, :], in_=bv2.rearrange("(cb p) -> cb p", p=P))
+            nc.sync.dma_start(out=gamma_bf16[:], in_=gamma.partition_broadcast(P))
+
+        def spread_constants():
+            bias_ps = psum.tile([P, P], BF16, tag="bank")
+            nc.tensor.transpose(out=bias_ps[:], in_=bias_rows[:], identity=ident_bf16[:])
+            nc.vector.tensor_copy(out=bias_col[:], in_=bias_ps[:, 0:BLOCKS])
+            nc.vector.tensor_copy(out=gamma_col[:], in_=gamma_bf16[:])
 
         live = {}
         for b in range(B):
@@ -344,3 +346,7 @@ def tile_mvpam_module_mask_cascade_pb_t_kernel(
         with tc.manual_schedule():
             for slot in range(-LOAD_AHEAD, ALL_BLOCKS + BACK + 1):
                 one_slot(slot)
+                if slot == -LOAD_AHEAD:
+                    load_constants()
+                if slot == 1 - QUERIES_AHEAD:
+                    spread_constants()

@@ -26,18 +26,21 @@ ALL_BLOCKS = B * BLOCKS
 
 FLOPS = 2 * B * (C * C * N + N * D * N + C * N * N)
 
-LOAD_AHEAD = 12
-QUERIES_AHEAD = 6
-REGROUP_AHEAD = 4
-QUANTISE_OUT1_AHEAD = 2
-REGROUPED_BUFFERS = REGROUP_AHEAD - QUANTISE_OUT1_AHEAD
-VALUES = 2
-TRANSPOSE = 4
-LOAD_RESIDUAL = 4
+LOAD_OUT1_AHEAD = 16
+LOAD_AHEAD = 8
+QUERIES_AHEAD = 5
+REGROUP_AHEAD = 12
+QUANTISE_OUT1_AHEAD = 4
+VALUES = -1
+QUANTISE_VAL = 3
+E_WORDS = 3
+QUANTISE_E = 6
 ROW_FACTORS = 5
-QUANTISE_KEYS = 6
-ATTEND = 10
-BACK = 12
+LOAD_RESIDUAL = 0
+ATTEND = 8
+BACK = 11
+MERGE_MX = False
+EARLY = 8
 
 
 def block(i):
@@ -56,6 +59,30 @@ def starts_item(t):
     return is_block(t) and t % BLOCKS == 0
 
 
+def e_blocks(s):
+    due = []
+    if BLOCKS <= s < ALL_BLOCKS:
+        due.append(s)
+    if 0 <= s + EARLY < BLOCKS:
+        due.append(s + EARLY)
+    return due
+
+
+def e_items(s):
+    return [t // BLOCKS for t in e_blocks(s) if t % BLOCKS == 0]
+
+
+DRAIN = 12
+
+
+def residual_on_tensor(t):
+    return t % 2 == 0 and t < ALL_BLOCKS - DRAIN
+
+
+def scale_on_vector(t):
+    return False
+
+
 def tile_mvpam_module_mask_cascade_pb_t_kernel(
     tc, x, out1, q, k, wv2_words, wv2_scales, bv2, gamma, out
 ):
@@ -63,9 +90,10 @@ def tile_mvpam_module_mask_cascade_pb_t_kernel(
     with ExitStack() as ctx:
         const = ctx.enter_context(tc.tile_pool(name="const", bufs=1))
         loads = ctx.enter_context(tc.tile_pool(name="loads", bufs=4))
+        raw = ctx.enter_context(tc.tile_pool(name="raw", bufs=3))
         work = ctx.enter_context(tc.tile_pool(name="work", bufs=3))
-        regrouped = ctx.enter_context(tc.tile_pool(name="regrouped", bufs=REGROUPED_BUFFERS))
-        results = ctx.enter_context(tc.tile_pool(name="results", bufs=4))
+        regrouped = ctx.enter_context(tc.tile_pool(name="regrouped", bufs=2))
+        results = ctx.enter_context(tc.tile_pool(name="results", bufs=6))
         psum = ctx.enter_context(tc.psum_pool(name="psum", bufs=8))
 
         ident_bf16 = const.tile([P, P], BF16)
@@ -76,9 +104,7 @@ def tile_mvpam_module_mask_cascade_pb_t_kernel(
         w_codes = const.tile([P, C], U32, align_bytes=64)
         w_scales = const.tile([P, C], U8, align_bytes=64)
         nc.vector.memset(w_scales[:].bitcast(I32), 0)
-        bias_rows = const.tile([P, P], BF16)
-        nc.vector.memset(bias_rows[:], 0.0)
-        bias_col = const.tile([P, BLOCKS], F32)
+        bias_row = const.tile([P, C], BF16)
         gamma_bf16 = const.tile([P, 1], BF16)
         gamma_col = const.tile([P, 1], F32)
 
@@ -92,13 +118,9 @@ def tile_mvpam_module_mask_cascade_pb_t_kernel(
                     out=w_scales[32 * quadrant : 32 * quadrant + 4, :].bitcast(I32),
                     in_=wv2_scales[0, 4 * quadrant : 4 * quadrant + 4, :].bitcast(I32),
                 )
-            nc.sync.dma_start(out=bias_rows[0:BLOCKS, :], in_=bv2.rearrange("(cb p) -> cb p", p=P))
-            nc.sync.dma_start(out=gamma_bf16[:], in_=gamma.partition_broadcast(P))
+            nc.sync.dma_start(out=bias_row[:], in_=bv2.partition_broadcast(P))
 
         def spread_constants():
-            bias_ps = psum.tile([P, P], BF16, tag="bank")
-            nc.tensor.transpose(out=bias_ps[:], in_=bias_rows[:], identity=ident_bf16[:])
-            nc.vector.tensor_copy(out=bias_col[:], in_=bias_ps[:, 0:BLOCKS])
             nc.vector.tensor_copy(out=gamma_col[:], in_=gamma_bf16[:])
 
         live = {}
@@ -116,7 +138,9 @@ def tile_mvpam_module_mask_cascade_pb_t_kernel(
             nc.sync.dma_start(out=q_sb[:], in_=q[b].rearrange("(mb p) d -> p mb d", p=P))
             k_sb = item_tile(loads, b, "k_sb", [D, N], BF16)
             nc.sync.dma_start(out=k_sb[:], in_=k[b])
-            o1_raw = item_tile(loads, b, "o1_raw", [P, PACK, N], BF16)
+
+        def load_out1(b):
+            o1_raw = item_tile(raw, b, "o1_raw", [P, PACK, N], BF16)
             nc.sync.dma_start(out=o1_raw[:], in_=out1[b].rearrange("(p j) n -> p j n", j=PACK))
 
         def load_residual(b):
@@ -133,7 +157,7 @@ def tile_mvpam_module_mask_cascade_pb_t_kernel(
 
         def copy_queries(b):
             qT_sb = item_tile(work, b, "qT_sb", [D, N], BF16)
-            nc.vector.tensor_copy(out=qT_sb[:], in_=banks["qT", b][:])
+            nc.scalar.copy(out=qT_sb[:], in_=banks["qT", b][:])
 
         def scores_matmul(t):
             b, mb = divmod(t, BLOCKS)
@@ -167,98 +191,90 @@ def tile_mvpam_module_mask_cascade_pb_t_kernel(
                 accum_out=row_sum[:, mb : mb + 1],
             )
 
-        def regroup_out1(t):
-            b, nb = divmod(t, BLOCKS)
-            o1_grouped = regrouped.tile([P, P, PACK], BF16, align_bytes=64)
-            nc.gpsimd.tensor_scalar(
-                out=o1_grouped[:],
-                in0=live[b]["o1_raw"][:, :, block(nb)].rearrange("p j n -> p n j"),
-                scalar1=1.0,
-                scalar2=0.0,
-                op0=ALU.mult,
-                op1=ALU.add,
-            )
-            banks["o1_grouped", t] = o1_grouped
+        def regroup_out1(b):
+            o1_grouped = regrouped.tile([P, PACK, P, PACK], BF16, align_bytes=64)
+            for u in range(PAIR):
+                nc.gpsimd.tensor_scalar(
+                    out=o1_grouped[:, 2 * u : 2 * u + 2, :, :],
+                    in0=live[b]["o1_raw"][:, :, half(u)].rearrange("p j (w h) -> p h w j", h=PAIR),
+                    scalar1=1.0,
+                    scalar2=0.0,
+                    op0=ALU.mult,
+                    op1=ALU.add,
+                )
+            banks["o1_grouped", b] = o1_grouped
 
-        def quantise_out1(t):
-            b, nb = divmod(t, BLOCKS)
+        def quantise_out1(b):
             o1_codes = item_tile(work, b, "o1_codes", [P, N], U32)
             o1_scales = item_tile(work, b, "o1_scales", [P, N], U8)
             nc.vector.quantize_mx(
-                out=o1_codes[:, block(nb)].bitcast(FP8X4),
-                scales=o1_scales[:, block(nb)],
-                in_=banks["o1_grouped", t][:].rearrange("p n j -> p (n j)"),
+                out=o1_codes[:].bitcast(FP8X4),
+                scales=o1_scales[:],
+                in_=banks["o1_grouped", b][:].rearrange("p t w j -> p (t w j)"),
             )
 
         def values_matmul(t):
             b, cb = divmod(t, BLOCKS)
-            val_ps = psum.tile([P, N], F32, tag="bank")
-            nc.tensor.matmul_mx(
-                out=val_ps[:],
-                lhsT=w_codes[:, block(cb)].bitcast(FP8X4),
-                lhsT_scale=w_scales[:, block(cb)],
-                rhs=live[b]["o1_codes"][:].bitcast(FP8X4),
-                rhs_scale=live[b]["o1_scales"][:],
-                start=True,
-                stop=True,
-            )
+            val_ps = psum.tile([P, PACK, P], F32, tag="bank")
+            for slot_of_word in range(PACK):
+                nc.tensor.matmul_mx(
+                    out=val_ps[:, slot_of_word, :],
+                    lhsT=live[b]["o1_codes"][:, block(slot_of_word)].bitcast(FP8X4),
+                    lhsT_scale=live[b]["o1_scales"][:, block(slot_of_word)],
+                    rhs=w_codes[:, block(cb)].bitcast(FP8X4),
+                    rhs_scale=w_scales[:, block(cb)],
+                    start=True,
+                    stop=True,
+                )
             banks["val", t] = val_ps
 
         def add_bias(t):
             b, cb = divmod(t, BLOCKS)
-            val_sb = item_tile(work, b, "val_sb", [P, BLOCKS, N], BF16)
-            nc.scalar.activation(
-                out=val_sb[:, cb, :],
-                in_=banks["val", t][:],
-                func=ACT.Identity,
-                bias=bias_col[:, cb : cb + 1],
-                scale=1.0,
+            val_grouped = item_tile(work, b, "val_grouped", [P, C, PACK], BF16)
+            nc.vector.tensor_tensor(
+                out=val_grouped[:, block(cb), :],
+                in0=banks["val", t][:].rearrange("p t c -> p c t"),
+                in1=bias_row[:, block(cb)].unsqueeze(2).to_broadcast([P, P, PACK]),
+                op=ALU.add,
             )
 
-        def matrix_and_half(t):
-            b, i = divmod(t, BLOCKS)
-            return b, ("e", "val")[i % 2], i // 2
-
-        def transpose_words(t):
-            b, matrix, h = matrix_and_half(t)
+        def transpose_words(b, h):
             words_ps = psum.tile([P, 2, PAIR, P], F32, tag="bank")
             for i in range(2):
-                row_words = live[b][matrix + "_sb"][:, 2 * h + i, :].bitcast(F32)
+                row_words = live[b]["e_sb"][:, 2 * h + i, :].bitcast(F32)
                 for u in range(PAIR):
                     nc.tensor.transpose(
                         out=words_ps[:, i, u, :], in_=row_words[:, block(u)], identity=ident_f32[:]
                     )
-            banks["words", t] = words_ps
+            banks["words", b, h] = words_ps
 
-        def copy_words(t):
-            b, matrix, h = matrix_and_half(t)
-            grouped = item_tile(work, b, matrix + "_grouped", [P, C, PACK], BF16)
+        def copy_words(b, h):
+            grouped = item_tile(work, b, "e_grouped", [P, C, PACK], BF16)
             grouped_words = (
                 grouped[:, half(h), :]
                 .rearrange("p r t -> p (r t)")
                 .bitcast(F32)
                 .rearrange("p (i r u) -> p i r u", i=2, u=PAIR)
             )
-            words = banks["words", t][:].rearrange("p i u r -> p i r u")
-            if matrix == "e":
-                nc.scalar.copy(out=grouped_words, in_=words)
-            else:
-                nc.vector.tensor_copy(out=grouped_words, in_=words)
+            words = banks["words", b, h][:].rearrange("p i u r -> p i r u")
+            nc.scalar.copy(out=grouped_words, in_=words)
 
-        def quantise_along_keys(t):
-            b, matrix, h = matrix_and_half(t)
+        def quantise_along_keys(b, matrix):
             codes = item_tile(work, b, matrix + "_codes", [P, C], U32)
             scales = item_tile(work, b, matrix + "_scales", [P, C], U8)
             nc.vector.quantize_mx(
-                out=codes[:, half(h)].bitcast(FP8X4),
-                scales=scales[:, half(h)],
-                in_=live[b][matrix + "_grouped"][:, half(h), :].rearrange("p r t -> p (r t)"),
+                out=codes[:].bitcast(FP8X4),
+                scales=scales[:],
+                in_=live[b][matrix + "_grouped"][:].rearrange("p r t -> p (r t)"),
             )
 
         def row_factors(b):
+            r_inv = item_tile(work, b, "r_inv", [P, BLOCKS], F32)
+            nc.vector.reciprocal(out=r_inv[:], in_=live[b]["row_sum"][:])
             r_col = item_tile(work, b, "r_col", [P, BLOCKS], F32)
-            nc.vector.reciprocal(out=r_col[:], in_=live[b]["row_sum"][:])
-            nc.vector.tensor_scalar_mul(out=r_col[:], in0=r_col[:], scalar1=gamma_col[:, 0:1])
+            nc.gpsimd.tensor_scalar(
+                out=r_col[:], in0=r_inv[:], scalar1=gamma_col[:, 0:1], scalar2=0.0, op0=ALU.mult, op1=ALU.add
+            )
 
         def attend_matmul(t):
             b, mb = divmod(t, BLOCKS)
@@ -277,76 +293,135 @@ def tile_mvpam_module_mask_cascade_pb_t_kernel(
         def scale_rows(t):
             b, mb = divmod(t, BLOCKS)
             scaled = results.tile([P, C], F32)
-            nc.scalar.activation(
-                out=scaled[:],
-                in_=banks["att", t][:],
-                func=ACT.Copy,
-                scale=live[b]["r_col"][:, mb : mb + 1],
-            )
+            if scale_on_vector(t):
+                nc.vector.tensor_scalar_mul(
+                    out=scaled[:], in0=banks["att", t][:], scalar1=live[b]["r_col"][:, mb : mb + 1]
+                )
+            else:
+                nc.scalar.activation(
+                    out=scaled[:],
+                    in_=banks["att", t][:],
+                    func=ACT.Copy,
+                    scale=live[b]["r_col"][:, mb : mb + 1],
+                )
             banks["scaled", t] = scaled
 
         def transpose_back(t):
+            b, mb = divmod(t, BLOCKS)
             o_ps = psum.tile([P, BLOCKS, P], F32, tag="bank")
-            for cb in range(BLOCKS):
-                nc.tensor.transpose(
-                    out=o_ps[:, cb, :], in_=banks["scaled", t][:, block(cb)], identity=ident_f32[:]
+            if residual_on_tensor(t):
+                nc.tensor.matmul(
+                    out=o_ps[:],
+                    lhsT=ident_bf16[:],
+                    rhs=live[b]["x_sb"][:, :, block(mb)],
+                    start=True,
+                    stop=False,
                 )
+                for cb in range(BLOCKS):
+                    nc.tensor.matmul(
+                        out=o_ps[:, cb, :],
+                        lhsT=banks["scaled", t][:, block(cb)],
+                        rhs=ident_f32[:],
+                        is_transpose=True,
+                        start=False,
+                        stop=(cb == BLOCKS - 1),
+                    )
+            else:
+                for cb in range(BLOCKS):
+                    nc.tensor.transpose(
+                        out=o_ps[:, cb, :], in_=banks["scaled", t][:, block(cb)], identity=ident_f32[:]
+                    )
             banks["o", t] = o_ps
 
         def add_residual(t):
             b, mb = divmod(t, BLOCKS)
             o_sb = results.tile([P, BLOCKS, P], F32)
-            nc.vector.tensor_tensor(
-                out=o_sb[:], in0=banks["o", t][:], in1=live[b]["x_sb"][:, :, block(mb)], op=ALU.add
-            )
+            if residual_on_tensor(t):
+                nc.scalar.copy(out=o_sb[:], in_=banks["o", t][:])
+            else:
+                nc.vector.tensor_tensor(
+                    out=o_sb[:], in0=banks["o", t][:], in1=live[b]["x_sb"][:, :, block(mb)], op=ALU.add
+                )
             nc.sync.dma_start(
                 out=out[b].rearrange("(cb p) m -> p cb m", p=P)[:, :, block(mb)], in_=o_sb[:]
             )
 
+        def e_half_due(slot):
+            return [(t // BLOCKS, (t % BLOCKS) // 2) for t in e_blocks(slot) if t % 2 == 0]
+
         def one_slot(slot):
-            if starts_item(slot + LOAD_AHEAD):
-                load_front((slot + LOAD_AHEAD) // BLOCKS)
+            for b in e_items(slot + LOAD_AHEAD):
+                if b > 0:
+                    load_front(b)
+            if starts_item(slot + LOAD_OUT1_AHEAD):
+                load_out1((slot + LOAD_OUT1_AHEAD) // BLOCKS)
             if starts_item(slot - LOAD_RESIDUAL):
                 load_residual((slot - LOAD_RESIDUAL) // BLOCKS)
-            if is_block(slot - 1 - TRANSPOSE):
-                copy_words(slot - 1 - TRANSPOSE)
-            if is_block(slot - 1):
-                exponentials(slot - 1)
-            if is_block(slot - 1 - BACK):
-                add_residual(slot - 1 - BACK)
-            if is_block(slot - 1 - VALUES):
-                add_bias(slot - 1 - VALUES)
-            if is_block(slot - 1 - ATTEND):
-                scale_rows(slot - 1 - ATTEND)
-            if starts_item(slot - 1 + QUERIES_AHEAD):
-                copy_queries((slot - 1 + QUERIES_AHEAD) // BLOCKS)
-            if is_block(slot):
-                scores_matmul(slot)
-            if is_block(slot - TRANSPOSE):
-                transpose_words(slot - TRANSPOSE)
-            if is_block(slot - BACK):
-                transpose_back(slot - BACK)
-            if starts_item(slot + QUERIES_AHEAD):
-                transpose_queries((slot + QUERIES_AHEAD) // BLOCKS)
-            if is_block(slot - VALUES):
-                values_matmul(slot - VALUES)
-            if is_block(slot - ATTEND):
-                attend_matmul(slot - ATTEND)
-            if is_block(slot):
-                row_maximum(slot)
-            if starts_item(slot - ROW_FACTORS):
-                row_factors((slot - ROW_FACTORS) // BLOCKS)
-            if is_block(slot - QUANTISE_KEYS):
-                quantise_along_keys(slot - QUANTISE_KEYS)
-            if is_block(slot + QUANTISE_OUT1_AHEAD):
-                quantise_out1(slot + QUANTISE_OUT1_AHEAD)
-            if is_block(slot + REGROUP_AHEAD):
-                regroup_out1(slot + REGROUP_AHEAD)
+
+            def empty_plain():
+                for b, h in e_half_due(slot - 1 - E_WORDS):
+                    copy_words(b, h)
+                for t in e_blocks(slot - 1):
+                    exponentials(t)
+                if is_block(slot - 1 - BACK):
+                    add_residual(slot - 1 - BACK)
+                for b in e_items(slot - 1 + QUERIES_AHEAD):
+                    copy_queries(b)
+
+            def empty_mx():
+                if is_block(slot - 1 - VALUES):
+                    add_bias(slot - 1 - VALUES)
+                if is_block(slot - 1 - ATTEND):
+                    scale_rows(slot - 1 - ATTEND)
+
+            def fill_plain():
+                for t in e_blocks(slot):
+                    scores_matmul(t)
+                for b, h in e_half_due(slot - E_WORDS):
+                    transpose_words(b, h)
+                if is_block(slot - BACK):
+                    transpose_back(slot - BACK)
+                for b in e_items(slot + QUERIES_AHEAD):
+                    transpose_queries(b)
+
+            def fill_mx():
+                if is_block(slot - VALUES):
+                    values_matmul(slot - VALUES)
+                if is_block(slot - ATTEND):
+                    attend_matmul(slot - ATTEND)
+
+            if MERGE_MX and slot % 2 == 1:
+                empty_plain()
+                empty_mx()
+                fill_mx()
+                fill_plain()
+            else:
+                if MERGE_MX:
+                    empty_mx()
+                    empty_plain()
+                else:
+                    empty_plain()
+                    empty_mx()
+                fill_plain()
+                fill_mx()
+            for t in e_blocks(slot):
+                row_maximum(t)
+            for b in e_items(slot - ROW_FACTORS):
+                row_factors(b)
+            for b in e_items(slot - QUANTISE_E):
+                quantise_along_keys(b, "e")
+            if starts_item(slot - QUANTISE_VAL):
+                quantise_along_keys((slot - QUANTISE_VAL) // BLOCKS, "val")
+            if starts_item(slot + QUANTISE_OUT1_AHEAD):
+                quantise_out1((slot + QUANTISE_OUT1_AHEAD) // BLOCKS)
+            if starts_item(slot + REGROUP_AHEAD):
+                regroup_out1((slot + REGROUP_AHEAD) // BLOCKS)
 
         with tc.manual_schedule():
-            for slot in range(-LOAD_AHEAD, ALL_BLOCKS + BACK + 1):
+            nc.sync.dma_start(out=gamma_bf16[:], in_=gamma.partition_broadcast(P))
+            load_front(0)
+            spread_constants()
+            for slot in range(-LOAD_OUT1_AHEAD, ALL_BLOCKS + BACK + 1):
                 one_slot(slot)
-                if slot == -LOAD_AHEAD:
+                if slot == -LOAD_OUT1_AHEAD:
                     load_constants()
-                if slot == 1 - QUERIES_AHEAD:
-                    spread_constants()

@@ -27,18 +27,18 @@ ALL_BLOCKS = B * BLOCKS
 FLOPS = 2 * B * (C * C * N + N * D * N + C * N * N)
 
 LOAD_OUT1_AHEAD = 16
-LOAD_AHEAD = 8
+LOAD_AHEAD = 12
 QUERIES_AHEAD = 5
-REGROUP_AHEAD = 12
+REGROUP_AHEAD = 8
 QUANTISE_OUT1_AHEAD = 4
 VALUES = -1
-QUANTISE_VAL = 3
+QUANTISE_VAL = 4
 E_WORDS = 3
-QUANTISE_E = 6
-ROW_FACTORS = 5
-LOAD_RESIDUAL = 0
-ATTEND = 8
-BACK = 11
+QUANTISE_E = 7
+ROW_FACTORS = 7
+LOAD_RESIDUAL = 4
+ATTEND = 9
+BACK = 12
 MERGE_MX = False
 EARLY = 8
 
@@ -92,7 +92,7 @@ def tile_mvpam_module_mask_cascade_pb_t_kernel(
         loads = ctx.enter_context(tc.tile_pool(name="loads", bufs=4))
         raw = ctx.enter_context(tc.tile_pool(name="raw", bufs=3))
         work = ctx.enter_context(tc.tile_pool(name="work", bufs=3))
-        regrouped = ctx.enter_context(tc.tile_pool(name="regrouped", bufs=2))
+        regrouped = ctx.enter_context(tc.tile_pool(name="regrouped", bufs=1))
         results = ctx.enter_context(tc.tile_pool(name="results", bufs=6))
         psum = ctx.enter_context(tc.psum_pool(name="psum", bufs=8))
 
@@ -271,10 +271,10 @@ def tile_mvpam_module_mask_cascade_pb_t_kernel(
         def row_factors(b):
             r_inv = item_tile(work, b, "r_inv", [P, BLOCKS], F32)
             nc.vector.reciprocal(out=r_inv[:], in_=live[b]["row_sum"][:])
+
+        def times_gamma(b):
             r_col = item_tile(work, b, "r_col", [P, BLOCKS], F32)
-            nc.gpsimd.tensor_scalar(
-                out=r_col[:], in0=r_inv[:], scalar1=gamma_col[:, 0:1], scalar2=0.0, op0=ALU.mult, op1=ALU.add
-            )
+            nc.scalar.activation(out=r_col[:], in_=live[b]["r_inv"][:], func=ACT.Copy, scale=gamma_col[:, 0:1])
 
         def attend_matmul(t):
             b, mb = divmod(t, BLOCKS)
@@ -404,6 +404,8 @@ def tile_mvpam_module_mask_cascade_pb_t_kernel(
                     empty_mx()
                 fill_plain()
                 fill_mx()
+            for b in e_items(slot - 1 - ROW_FACTORS):
+                times_gamma(b)
             for t in e_blocks(slot):
                 row_maximum(t)
             for b in e_items(slot - ROW_FACTORS):

@@ -29,18 +29,20 @@ FLOPS = 2 * B * (C * C * N + N * D * N + C * N * N)
 LOAD_OUT1_AHEAD = 16
 LOAD_AHEAD = 12
 QUERIES_AHEAD = 5
-REGROUP_AHEAD = 8
-QUANTISE_OUT1_AHEAD = 4
+REGROUP_AHEAD = 9
+QUANTISE_OUT1_AHEAD = 5
 VALUES = -1
-QUANTISE_VAL = 4
+QUANTISE_VAL = 3
 E_WORDS = 3
-QUANTISE_E = 7
-ROW_FACTORS = 7
+QUANTISE_E = 6
+ROW_FACTORS = 6
 LOAD_RESIDUAL = 4
-ATTEND = 9
-BACK = 12
+ATTEND = 7
+BACK = 9
 MERGE_MX = False
-EARLY = 8
+EARLY_V = 2
+EARLY_Q = 4
+EARLY = 4
 
 
 def block(i):
@@ -66,6 +68,23 @@ def e_blocks(s):
     if 0 <= s + EARLY < BLOCKS:
         due.append(s + EARLY)
     return due
+
+
+def v_blocks(s):
+    due = []
+    if BLOCKS <= s < ALL_BLOCKS:
+        due.append(s)
+    if 0 <= s + EARLY_V < BLOCKS:
+        due.append(s + EARLY_V)
+    return due
+
+
+def late_e_items(s):
+    if s + EARLY_Q == 0:
+        return [0]
+    if s > 0 and starts_item(s):
+        return [s // BLOCKS]
+    return []
 
 
 def e_items(s):
@@ -194,14 +213,20 @@ def tile_mvpam_module_mask_cascade_pb_t_kernel(
         def regroup_out1(b):
             o1_grouped = regrouped.tile([P, PACK, P, PACK], BF16, align_bytes=64)
             for u in range(PAIR):
-                nc.gpsimd.tensor_scalar(
-                    out=o1_grouped[:, 2 * u : 2 * u + 2, :, :],
-                    in0=live[b]["o1_raw"][:, :, half(u)].rearrange("p j (w h) -> p h w j", h=PAIR),
-                    scalar1=1.0,
-                    scalar2=0.0,
-                    op0=ALU.mult,
-                    op1=ALU.add,
-                )
+                if b == 0:
+                    nc.vector.tensor_copy(
+                        out=o1_grouped[:, 2 * u : 2 * u + 2, :, :],
+                        in_=live[b]["o1_raw"][:, :, half(u)].rearrange("p j (w h) -> p h w j", h=PAIR),
+                    )
+                else:
+                    nc.gpsimd.tensor_scalar(
+                        out=o1_grouped[:, 2 * u : 2 * u + 2, :, :],
+                        in0=live[b]["o1_raw"][:, :, half(u)].rearrange("p j (w h) -> p h w j", h=PAIR),
+                        scalar1=1.0,
+                        scalar2=0.0,
+                        op0=ALU.mult,
+                        op1=ALU.add,
+                    )
             banks["o1_grouped", b] = o1_grouped
 
         def quantise_out1(b):
@@ -353,7 +378,7 @@ def tile_mvpam_module_mask_cascade_pb_t_kernel(
             for b in e_items(slot + LOAD_AHEAD):
                 if b > 0:
                     load_front(b)
-            if starts_item(slot + LOAD_OUT1_AHEAD):
+            if starts_item(slot + LOAD_OUT1_AHEAD) and slot + LOAD_OUT1_AHEAD > 0:
                 load_out1((slot + LOAD_OUT1_AHEAD) // BLOCKS)
             if starts_item(slot - LOAD_RESIDUAL):
                 load_residual((slot - LOAD_RESIDUAL) // BLOCKS)
@@ -369,8 +394,8 @@ def tile_mvpam_module_mask_cascade_pb_t_kernel(
                     copy_queries(b)
 
             def empty_mx():
-                if is_block(slot - 1 - VALUES):
-                    add_bias(slot - 1 - VALUES)
+                for t in v_blocks(slot - 1 - VALUES):
+                    add_bias(t)
                 if is_block(slot - 1 - ATTEND):
                     scale_rows(slot - 1 - ATTEND)
 
@@ -385,8 +410,8 @@ def tile_mvpam_module_mask_cascade_pb_t_kernel(
                     transpose_queries(b)
 
             def fill_mx():
-                if is_block(slot - VALUES):
-                    values_matmul(slot - VALUES)
+                for t in v_blocks(slot - VALUES):
+                    values_matmul(t)
                 if is_block(slot - ATTEND):
                     attend_matmul(slot - ATTEND)
 
@@ -404,26 +429,28 @@ def tile_mvpam_module_mask_cascade_pb_t_kernel(
                     empty_mx()
                 fill_plain()
                 fill_mx()
-            for b in e_items(slot - 1 - ROW_FACTORS):
+            for b in late_e_items(slot - 1 - ROW_FACTORS):
                 times_gamma(b)
             for t in e_blocks(slot):
                 row_maximum(t)
-            for b in e_items(slot - ROW_FACTORS):
+            for b in late_e_items(slot - ROW_FACTORS):
                 row_factors(b)
-            for b in e_items(slot - QUANTISE_E):
+            for b in late_e_items(slot - QUANTISE_E):
                 quantise_along_keys(b, "e")
             if starts_item(slot - QUANTISE_VAL):
                 quantise_along_keys((slot - QUANTISE_VAL) // BLOCKS, "val")
-            if starts_item(slot + QUANTISE_OUT1_AHEAD):
+            if starts_item(slot + QUANTISE_OUT1_AHEAD) and slot + QUANTISE_OUT1_AHEAD > 0:
                 quantise_out1((slot + QUANTISE_OUT1_AHEAD) // BLOCKS)
-            if starts_item(slot + REGROUP_AHEAD):
+            if starts_item(slot + REGROUP_AHEAD) and slot + REGROUP_AHEAD > 0:
                 regroup_out1((slot + REGROUP_AHEAD) // BLOCKS)
 
         with tc.manual_schedule():
             nc.sync.dma_start(out=gamma_bf16[:], in_=gamma.partition_broadcast(P))
+            load_out1(0)
             load_front(0)
+            load_constants()
             spread_constants()
+            regroup_out1(0)
+            quantise_out1(0)
             for slot in range(-LOAD_OUT1_AHEAD, ALL_BLOCKS + BACK + 1):
                 one_slot(slot)
-                if slot == -LOAD_OUT1_AHEAD:
-                    load_constants()

@@ -91,7 +91,7 @@ def e_items(s):
     return [t // BLOCKS for t in e_blocks(s) if t % BLOCKS == 0]
 
 
-DRAIN = 12
+DRAIN = 0
 
 
 def residual_on_tensor(t):

@@ -28,17 +28,17 @@ FLOPS = 2 * B * (C * C * N + N * D * N + C * N * N)
 
 LOAD_OUT1_AHEAD = 16
 LOAD_AHEAD = 12
-QUERIES_AHEAD = 5
-REGROUP_AHEAD = 9
-QUANTISE_OUT1_AHEAD = 5
+QUERIES_AHEAD = 4
+REGROUP_AHEAD = 8
+QUANTISE_OUT1_AHEAD = 4
 VALUES = -1
-QUANTISE_VAL = 3
-E_WORDS = 3
-QUANTISE_E = 6
-ROW_FACTORS = 6
+QUANTISE_VAL = 4
+E_WORDS = 4
+QUANTISE_E = 7
+ROW_FACTORS = 7
 LOAD_RESIDUAL = 4
-ATTEND = 7
-BACK = 9
+ATTEND = 8
+BACK = 10
 MERGE_MX = False
 EARLY_V = 2
 EARLY_Q = 4
@@ -91,11 +91,12 @@ def e_items(s):
     return [t // BLOCKS for t in e_blocks(s) if t % BLOCKS == 0]
 
 
+TENSOR_ADDS = (0, 1)
 DRAIN = 0
 
 
 def residual_on_tensor(t):
-    return t % 2 == 0 and t < ALL_BLOCKS - DRAIN
+    return t % BLOCKS in TENSOR_ADDS and t < ALL_BLOCKS - DRAIN
 
 
 def scale_on_vector(t):
@@ -372,7 +373,7 @@ def tile_mvpam_module_mask_cascade_pb_t_kernel(
             )
 
         def e_half_due(slot):
-            return [(t // BLOCKS, (t % BLOCKS) // 2) for t in e_blocks(slot) if t % 2 == 0]
+            return [(t // BLOCKS, t % BLOCKS) for t in e_blocks(slot) if t % BLOCKS < 2]
 
         def one_slot(slot):
             for b in e_items(slot + LOAD_AHEAD):

from contextlib import ExitStack

import concourse.mybir as mybir
from concourse.masks import make_identity

BF16 = mybir.dt.bfloat16
F32 = mybir.dt.float32
I32 = mybir.dt.int32
U32 = mybir.dt.uint32
U8 = mybir.dt.uint8
FP8X4 = mybir.dt.float8_e4m3fn_x4
ACT = mybir.ActivationFunctionType
ALU = mybir.AluOpType
AXIS = mybir.AxisListType

B = 16
C = 512
N = 512
D = 128
P = 128
PACK = 4
PAIR = 2
BLOCKS = C // P
HALF = C // 2
ALL_BLOCKS = B * BLOCKS

FLOPS = 2 * B * (C * C * N + N * D * N + C * N * N)

LOAD_OUT1_AHEAD = 16
LOAD_AHEAD = 12
QUERIES_AHEAD = 4
REGROUP_AHEAD = 8
QUANTISE_OUT1_AHEAD = 4
VALUES = -1
QUANTISE_VAL = 4
E_WORDS = 4
QUANTISE_E = 7
ROW_FACTORS = 7
LOAD_RESIDUAL = 4
ATTEND = 8
BACK = 10
MERGE_MX = False
EARLY_V = 2
EARLY_Q = 4
EARLY = 4


def block(i):
    return slice(i * P, (i + 1) * P)


def half(h):
    return slice(h * HALF, (h + 1) * HALF)


def is_block(t):
    return 0 <= t < ALL_BLOCKS


def starts_item(t):
    return is_block(t) and t % BLOCKS == 0


def e_blocks(s):
    due = []
    if BLOCKS <= s < ALL_BLOCKS:
        due.append(s)
    if 0 <= s + EARLY < BLOCKS:
        due.append(s + EARLY)
    return due


def v_blocks(s):
    due = []
    if BLOCKS <= s < ALL_BLOCKS:
        due.append(s)
    if 0 <= s + EARLY_V < BLOCKS:
        due.append(s + EARLY_V)
    return due


def late_e_items(s):
    if s + EARLY_Q == 0:
        return [0]
    if s > 0 and starts_item(s):
        return [s // BLOCKS]
    return []


def e_items(s):
    return [t // BLOCKS for t in e_blocks(s) if t % BLOCKS == 0]


TENSOR_ADDS = (0, 1)
DRAIN = 0


def residual_on_tensor(t):
    return t % BLOCKS in TENSOR_ADDS and t < ALL_BLOCKS - DRAIN


def scale_on_vector(t):
    return False


def tile_mvpam_module_mask_cascade_pb_t_kernel(
    tc, x, out1, q, k, wv2_words, wv2_scales, bv2, gamma, out
):
    nc = tc.nc
    with ExitStack() as ctx:
        const = ctx.enter_context(tc.tile_pool(name="const", bufs=1))
        loads = ctx.enter_context(tc.tile_pool(name="loads", bufs=4))
        raw = ctx.enter_context(tc.tile_pool(name="raw", bufs=3))
        work = ctx.enter_context(tc.tile_pool(name="work", bufs=3))
        regrouped = ctx.enter_context(tc.tile_pool(name="regrouped", bufs=1))
        results = ctx.enter_context(tc.tile_pool(name="results", bufs=6))
        psum = ctx.enter_context(tc.psum_pool(name="psum", bufs=8))

        ident_bf16 = const.tile([P, P], BF16)
        make_identity(nc, ident_bf16[:])
        ident_f32 = const.tile([P, P], F32)
        make_identity(nc, ident_f32[:])

        w_codes = const.tile([P, C], U32, align_bytes=64)
        w_scales = const.tile([P, C], U8, align_bytes=64)
        nc.vector.memset(w_scales[:].bitcast(I32), 0)
        bias_row = const.tile([P, C], BF16)
        gamma_bf16 = const.tile([P, 1], BF16)
        gamma_col = const.tile([P, 1], F32)

        def load_constants():
            nc.sync.dma_start(
                out=w_codes[:].bitcast(I32),
                in_=wv2_words[0].rearrange("p c t -> p (c t)").bitcast(I32),
            )
            for quadrant in range(4):
                nc.sync.dma_start(
                    out=w_scales[32 * quadrant : 32 * quadrant + 4, :].bitcast(I32),
                    in_=wv2_scales[0, 4 * quadrant : 4 * quadrant + 4, :].bitcast(I32),
                )
            nc.sync.dma_start(out=bias_row[:], in_=bv2.partition_broadcast(P))

        def spread_constants():
            nc.vector.tensor_copy(out=gamma_col[:], in_=gamma_bf16[:])

        live = {}
        for b in range(B):
            live[b] = {}
        banks = {}

        def item_tile(pool, b, name, shape, dtype):
            if name not in live[b]:
                live[b][name] = pool.tile(shape, dtype, name=name, align_bytes=64)
            return live[b][name]

        def load_front(b):
            q_sb = item_tile(loads, b, "q_sb", [P, BLOCKS, D], BF16)
            nc.sync.dma_start(out=q_sb[:], in_=q[b].rearrange("(mb p) d -> p mb d", p=P))
            k_sb = item_tile(loads, b, "k_sb", [D, N], BF16)
            nc.sync.dma_start(out=k_sb[:], in_=k[b])

        def load_out1(b):
            o1_raw = item_tile(raw, b, "o1_raw", [P, PACK, N], BF16)
            nc.sync.dma_start(out=o1_raw[:], in_=out1[b].rearrange("(p j) n -> p j n", j=PACK))

        def load_residual(b):
            x_sb = item_tile(loads, b, "x_sb", [P, BLOCKS, N], BF16)
            nc.sync.dma_start(out=x_sb[:], in_=x[b].rearrange("(cb p) m -> p cb m", p=P))

        def transpose_queries(b):
            qT_ps = psum.tile([D, N], BF16, tag="bank")
            for mb in range(BLOCKS):
                nc.tensor.transpose(
                    out=qT_ps[:, block(mb)], in_=live[b]["q_sb"][:, mb, :], identity=ident_bf16[:]
                )
            banks["qT", b] = qT_ps

        def copy_queries(b):
            qT_sb = item_tile(work, b, "qT_sb", [D, N], BF16)
            nc.scalar.copy(out=qT_sb[:], in_=banks["qT", b][:])

        def scores_matmul(t):
            b, mb = divmod(t, BLOCKS)
            s_ps = psum.tile([P, N], F32, tag="bank")
            nc.tensor.matmul(
                out=s_ps[:],
                lhsT=live[b]["qT_sb"][:, block(mb)],
                rhs=live[b]["k_sb"][:],
                start=True,
                stop=True,
            )
            banks["s", t] = s_ps

        def row_maximum(t):
            b, mb = divmod(t, BLOCKS)
            neg_max = item_tile(work, b, "neg_max", [P, BLOCKS], F32)
            nc.vector.tensor_reduce(
                out=neg_max[:, mb : mb + 1], in_=banks["s", t][:], axis=AXIS.X, op=ALU.max, negate=True
            )

        def exponentials(t):
            b, mb = divmod(t, BLOCKS)
            e_sb = item_tile(work, b, "e_sb", [P, BLOCKS, N], BF16)
            row_sum = item_tile(work, b, "row_sum", [P, BLOCKS], F32)
            nc.scalar.activation(
                out=e_sb[:, mb, :],
                in_=banks["s", t][:],
                func=ACT.Exp,
                bias=live[b]["neg_max"][:, mb : mb + 1],
                scale=1.0,
                accum_out=row_sum[:, mb : mb + 1],
            )

        def regroup_out1(b):
            o1_grouped = regrouped.tile([P, PACK, P, PACK], BF16, align_bytes=64)
            for u in range(PAIR):
                if b == 0:
                    nc.vector.tensor_copy(
                        out=o1_grouped[:, 2 * u : 2 * u + 2, :, :],
                        in_=live[b]["o1_raw"][:, :, half(u)].rearrange("p j (w h) -> p h w j", h=PAIR),
                    )
                else:
                    nc.gpsimd.tensor_scalar(
                        out=o1_grouped[:, 2 * u : 2 * u + 2, :, :],
                        in0=live[b]["o1_raw"][:, :, half(u)].rearrange("p j (w h) -> p h w j", h=PAIR),
                        scalar1=1.0,
                        scalar2=0.0,
                        op0=ALU.mult,
                        op1=ALU.add,
                    )
            banks["o1_grouped", b] = o1_grouped

        def quantise_out1(b):
            o1_codes = item_tile(work, b, "o1_codes", [P, N], U32)
            o1_scales = item_tile(work, b, "o1_scales", [P, N], U8)
            nc.vector.quantize_mx(
                out=o1_codes[:].bitcast(FP8X4),
                scales=o1_scales[:],
                in_=banks["o1_grouped", b][:].rearrange("p t w j -> p (t w j)"),
            )

        def values_matmul(t):
            b, cb = divmod(t, BLOCKS)
            val_ps = psum.tile([P, PACK, P], F32, tag="bank")
            for slot_of_word in range(PACK):
                nc.tensor.matmul_mx(
                    out=val_ps[:, slot_of_word, :],
                    lhsT=live[b]["o1_codes"][:, block(slot_of_word)].bitcast(FP8X4),
                    lhsT_scale=live[b]["o1_scales"][:, block(slot_of_word)],
                    rhs=w_codes[:, block(cb)].bitcast(FP8X4),
                    rhs_scale=w_scales[:, block(cb)],
                    start=True,
                    stop=True,
                )
            banks["val", t] = val_ps

        def add_bias(t):
            b, cb = divmod(t, BLOCKS)
            val_grouped = item_tile(work, b, "val_grouped", [P, C, PACK], BF16)
            nc.vector.tensor_tensor(
                out=val_grouped[:, block(cb), :],
                in0=banks["val", t][:].rearrange("p t c -> p c t"),
                in1=bias_row[:, block(cb)].unsqueeze(2).to_broadcast([P, P, PACK]),
                op=ALU.add,
            )

        def transpose_words(b, h):
            words_ps = psum.tile([P, 2, PAIR, P], F32, tag="bank")
            for i in range(2):
                row_words = live[b]["e_sb"][:, 2 * h + i, :].bitcast(F32)
                for u in range(PAIR):
                    nc.tensor.transpose(
                        out=words_ps[:, i, u, :], in_=row_words[:, block(u)], identity=ident_f32[:]
                    )
            banks["words", b, h] = words_ps

        def copy_words(b, h):
            grouped = item_tile(work, b, "e_grouped", [P, C, PACK], BF16)
            grouped_words = (
                grouped[:, half(h), :]
                .rearrange("p r t -> p (r t)")
                .bitcast(F32)
                .rearrange("p (i r u) -> p i r u", i=2, u=PAIR)
            )
            words = banks["words", b, h][:].rearrange("p i u r -> p i r u")
            nc.scalar.copy(out=grouped_words, in_=words)

        def quantise_along_keys(b, matrix):
            codes = item_tile(work, b, matrix + "_codes", [P, C], U32)
            scales = item_tile(work, b, matrix + "_scales", [P, C], U8)
            nc.vector.quantize_mx(
                out=codes[:].bitcast(FP8X4),
                scales=scales[:],
                in_=live[b][matrix + "_grouped"][:].rearrange("p r t -> p (r t)"),
            )

        def row_factors(b):
            r_inv = item_tile(work, b, "r_inv", [P, BLOCKS], F32)
            nc.vector.reciprocal(out=r_inv[:], in_=live[b]["row_sum"][:])

        def times_gamma(b):
            r_col = item_tile(work, b, "r_col", [P, BLOCKS], F32)
            nc.scalar.activation(out=r_col[:], in_=live[b]["r_inv"][:], func=ACT.Copy, scale=gamma_col[:, 0:1])

        def attend_matmul(t):
            b, mb = divmod(t, BLOCKS)
            att_ps = psum.tile([P, C], F32, tag="bank")
            nc.tensor.matmul_mx(
                out=att_ps[:],
                lhsT=live[b]["e_codes"][:, block(mb)].bitcast(FP8X4),
                lhsT_scale=live[b]["e_scales"][:, block(mb)],
                rhs=live[b]["val_codes"][:].bitcast(FP8X4),
                rhs_scale=live[b]["val_scales"][:],
                start=True,
                stop=True,
            )
            banks["att", t] = att_ps

        def scale_rows(t):
            b, mb = divmod(t, BLOCKS)
            scaled = results.tile([P, C], F32)
            if scale_on_vector(t):
                nc.vector.tensor_scalar_mul(
                    out=scaled[:], in0=banks["att", t][:], scalar1=live[b]["r_col"][:, mb : mb + 1]
                )
            else:
                nc.scalar.activation(
                    out=scaled[:],
                    in_=banks["att", t][:],
                    func=ACT.Copy,
                    scale=live[b]["r_col"][:, mb : mb + 1],
                )
            banks["scaled", t] = scaled

        def transpose_back(t):
            b, mb = divmod(t, BLOCKS)
            o_ps = psum.tile([P, BLOCKS, P], F32, tag="bank")
            if residual_on_tensor(t):
                nc.tensor.matmul(
                    out=o_ps[:],
                    lhsT=ident_bf16[:],
                    rhs=live[b]["x_sb"][:, :, block(mb)],
                    start=True,
                    stop=False,
                )
                for cb in range(BLOCKS):
                    nc.tensor.matmul(
                        out=o_ps[:, cb, :],
                        lhsT=banks["scaled", t][:, block(cb)],
                        rhs=ident_f32[:],
                        is_transpose=True,
                        start=False,
                        stop=(cb == BLOCKS - 1),
                    )
            else:
                for cb in range(BLOCKS):
                    nc.tensor.transpose(
                        out=o_ps[:, cb, :], in_=banks["scaled", t][:, block(cb)], identity=ident_f32[:]
                    )
            banks["o", t] = o_ps

        def add_residual(t):
            b, mb = divmod(t, BLOCKS)
            o_sb = results.tile([P, BLOCKS, P], F32)
            if residual_on_tensor(t):
                nc.scalar.copy(out=o_sb[:], in_=banks["o", t][:])
            else:
                nc.vector.tensor_tensor(
                    out=o_sb[:], in0=banks["o", t][:], in1=live[b]["x_sb"][:, :, block(mb)], op=ALU.add
                )
            nc.sync.dma_start(
                out=out[b].rearrange("(cb p) m -> p cb m", p=P)[:, :, block(mb)], in_=o_sb[:]
            )

        def e_half_due(slot):
            return [(t // BLOCKS, t % BLOCKS) for t in e_blocks(slot) if t % BLOCKS < 2]

        def one_slot(slot):
            for b in e_items(slot + LOAD_AHEAD):
                if b > 0:
                    load_front(b)
            if starts_item(slot + LOAD_OUT1_AHEAD) and slot + LOAD_OUT1_AHEAD > 0:
                load_out1((slot + LOAD_OUT1_AHEAD) // BLOCKS)
            if starts_item(slot - LOAD_RESIDUAL):
                load_residual((slot - LOAD_RESIDUAL) // BLOCKS)

            def empty_plain():
                for b, h in e_half_due(slot - 1 - E_WORDS):
                    copy_words(b, h)
                for t in e_blocks(slot - 1):
                    exponentials(t)
                if is_block(slot - 1 - BACK):
                    add_residual(slot - 1 - BACK)
                for b in e_items(slot - 1 + QUERIES_AHEAD):
                    copy_queries(b)

            def empty_mx():
                for t in v_blocks(slot - 1 - VALUES):
                    add_bias(t)
                if is_block(slot - 1 - ATTEND):
                    scale_rows(slot - 1 - ATTEND)

            def fill_plain():
                for t in e_blocks(slot):
                    scores_matmul(t)
                for b, h in e_half_due(slot - E_WORDS):
                    transpose_words(b, h)
                if is_block(slot - BACK):
                    transpose_back(slot - BACK)
                for b in e_items(slot + QUERIES_AHEAD):
                    transpose_queries(b)

            def fill_mx():
                for t in v_blocks(slot - VALUES):
                    values_matmul(t)
                if is_block(slot - ATTEND):
                    attend_matmul(slot - ATTEND)

            if MERGE_MX and slot % 2 == 1:
                empty_plain()
                empty_mx()
                fill_mx()
                fill_plain()
            else:
                if MERGE_MX:
                    empty_mx()
                    empty_plain()
                else:
                    empty_plain()
                    empty_mx()
                fill_plain()
                fill_mx()
            for b in late_e_items(slot - 1 - ROW_FACTORS):
                times_gamma(b)
            for t in e_blocks(slot):
                row_maximum(t)
            for b in late_e_items(slot - ROW_FACTORS):
                row_factors(b)
            for b in late_e_items(slot - QUANTISE_E):
                quantise_along_keys(b, "e")
            if starts_item(slot - QUANTISE_VAL):
                quantise_along_keys((slot - QUANTISE_VAL) // BLOCKS, "val")
            if starts_item(slot + QUANTISE_OUT1_AHEAD) and slot + QUANTISE_OUT1_AHEAD > 0:
                quantise_out1((slot + QUANTISE_OUT1_AHEAD) // BLOCKS)
            if starts_item(slot + REGROUP_AHEAD) and slot + REGROUP_AHEAD > 0:
                regroup_out1((slot + REGROUP_AHEAD) // BLOCKS)

        with tc.manual_schedule():
            nc.sync.dma_start(out=gamma_bf16[:], in_=gamma.partition_broadcast(P))
            load_out1(0)
            load_front(0)
            load_constants()
            spread_constants()
            regroup_out1(0)
            quantise_out1(0)
            for slot in range(-LOAD_OUT1_AHEAD, ALL_BLOCKS + BACK + 1):
                one_slot(slot)
